import numpy as np
import ml_dtypes


def mxq(x, axis, fmt="e4m3"):
    dtype, down = {"e4m3": (ml_dtypes.float8_e4m3fn, 7), "e5m2": (ml_dtypes.float8_e5m2, 14)}[fmt]
    v = np.moveaxis(np.asarray(x, np.float32).astype(ml_dtypes.bfloat16).astype(np.float64), axis, -1)
    blocks = v.reshape(v.shape[:-1] + (-1, 32))
    amax = np.abs(blocks).max(-1, keepdims=True)
    byte = np.maximum(np.where(amax > 0, np.frexp(amax)[1] - 1 + 127, 0) - down, 1)
    scale = np.exp2(byte - 127.0)
    codes = (blocks / scale).astype(np.float32).astype(dtype).astype(np.float64)
    return np.moveaxis((codes * scale).reshape(v.shape), -1, axis)


WIDE = False


def mx_kscale(k):
    if not WIDE:
        return np.ones(k)
    levels = np.array([10, -10, 5, -5, 0])
    a = np.random.permutation(np.resize(levels, k // 512 * 4)).reshape(k // 512, 4)
    idx = np.arange(k)
    return np.exp2(a[idx // 512, idx % 128 // 32])


BF16 = ml_dtypes.bfloat16


def bf(x):
    return np.asarray(x, np.float32).astype(BF16)


def f64(x):
    return np.asarray(x).astype(np.float64)


E2M1 = np.array([0.0, 0.5, 1.0, 1.5, 2.0, 3.0, 4.0, 6.0, -0.0, -0.5, -1.0, -1.5, -2.0, -3.0, -4.0, -6.0])


def pack_weight(w, fmt):
    k, n = w.shape
    w = f64(bf(w)).reshape(k // 32, 32, n)
    amax = np.abs(w).max(1)
    if fmt == "e4m3":
        byte = np.frexp(amax)[1] - 1 + 127 - 7
    else:
        mant, ex = np.frexp(amax / 6.0)
        byte = np.where(mant > 0.5, ex, ex - 1) + 127
    byte = np.clip(np.where(amax > 0, byte, 1), 1, 254)
    scaled = (w * np.exp2(127.0 - byte)[:, None, :]).reshape(k, n).astype(np.float32)
    by_word = np.ascontiguousarray(scaled.reshape(k // 512, 128, 4, n).transpose(0, 1, 3, 2))
    if fmt == "e4m3":
        words = by_word.astype(ml_dtypes.float8_e4m3fn).view(np.uint8)
    else:
        c = by_word.astype(ml_dtypes.float4_e2m1fn).view(np.uint8) & 0xF
        words = c[..., 0::2] | (c[..., 1::2] << 4)
    return np.ascontiguousarray(words), np.ascontiguousarray(byte.astype(np.uint8).reshape(k // 512, 16, n))


def unpack_weight(words, scales, fmt):
    g, p, n, _ = words.shape
    if fmt == "e4m3":
        vals = np.ascontiguousarray(words).view(ml_dtypes.float8_e4m3fn).astype(np.float64)
    else:
        nib = np.empty((g, p, n, 4), np.uint8)
        nib[..., 0::2] = words & 0xF
        nib[..., 1::2] = words >> 4
        vals = E2M1[nib]
    vals = vals * np.repeat(np.exp2(scales.astype(np.float64) - 127.0), 8, axis=1)[..., None]
    return vals.transpose(0, 1, 3, 2).reshape(g * 512, n)


B, L, C, K, D_MODEL, H, D_LLM = 64, 64, 2, 100, 512, 32, 1024
D_KEYS = D_MODEL // H
G = H * D_KEYS


def setup_inputs():
    s = mx_kscale(G).reshape(H, D_KEYS)
    attn_ctx = bf(np.random.standard_normal((B, C, L, H, D_KEYS)) * 0.5 * s)
    wo = np.random.standard_normal((C, H, D_KEYS, D_LLM)) * 2.0 / np.sqrt(G) / s[:, :, None]
    wo_words, wo_scales = pack_weight(wo.reshape(C, G, D_LLM).reshape(-1, D_LLM), "e4m3")
    bo = bf(np.random.standard_normal((C, D_LLM)) * 0.5)
    cluster_probs = bf(np.random.uniform(size=(B, L, C)))
    return {
        "attn_ctx": attn_ctx,
        "Wo_words": wo_words,
        "Wo_scales": wo_scales,
        "bo": bo,
        "cluster_probs": cluster_probs,
    }


def reference(attn_ctx, Wo_words, Wo_scales, bo, cluster_probs):
    o = f64(attn_ctx).reshape(B, C, L, G)
    w = unpack_weight(Wo_words, Wo_scales, "e4m3").reshape(C, G, D_LLM)
    proj = mxq(o, 3, "e4m3") @ w
    aligned = proj.transpose(0, 2, 1, 3) + f64(bo)
    return (aligned * f64(cluster_probs)[:, :, :, None]).sum(-2)

@@ -1,0 +1,162 @@
+from contextlib import ExitStack
+
+import concourse.mybir as mybir
+from concourse.masks import make_identity
+
+F32 = mybir.dt.float32
+BF16 = mybir.dt.bfloat16
+I32 = mybir.dt.int32
+U32 = mybir.dt.uint32
+U8 = mybir.dt.uint8
+FP8X4 = mybir.dt.float8_e4m3fn_x4
+MULT = mybir.AluOpType.mult
+ADD = mybir.AluOpType.add
+COPY = mybir.ActivationFunctionType.Copy
+
+P = 128
+BATCH, SEQ, CLUSTERS, K, E = 64, 64, 2, 512, 1024
+HALVES = 2
+N_TILES = SEQ // HALVES
+BANK = 512
+E_BANKS = E // BANK
+WORDS = K // 2
+CHUNK = 4
+STORE = 2
+
+FLOPS = 2 * BATCH * SEQ * CLUSTERS * K * E
+
+
+def tile_model_pa_t_e_kernel(tc, attn_ctx, Wo_words, Wo_scales, bo, cluster_probs, out):
+    nc = tc.nc
+
+    x_rows = attn_ctx.rearrange("b c (half j) h d -> (b c) half j (h d)", half=HALVES)
+    probs_rows = cluster_probs.rearrange("b (half j) c -> (b half) (j c)", half=HALVES)
+    out_rows = out.rearrange("b (half j) e -> (b half) j e", half=HALVES)
+
+    with ExitStack() as stack:
+        const = stack.enter_context(tc.tile_pool(name="const", bufs=1))
+        x_pool = stack.enter_context(tc.tile_pool(name="x", bufs=N_TILES // CHUNK))
+        quant = stack.enter_context(tc.tile_pool(name="quant", bufs=3))
+        bias_pool = stack.enter_context(tc.tile_pool(name="bias", bufs=4))
+        result = stack.enter_context(tc.tile_pool(name="result", bufs=3))
+        psum_x = stack.enter_context(tc.psum_pool(name="psum_x", bufs=2))
+        psum_acc = stack.enter_context(tc.psum_pool(name="psum_acc", bufs=6))
+
+        w_scales = const.tile([P, CLUSTERS, E], U8, align_bytes=64)
+        nc.vector.memset(w_scales[:].bitcast(I32), 0)
+        for quadrant in range(4):
+            nc.sync.dma_start(
+                out=w_scales[32 * quadrant : 32 * quadrant + 4].bitcast(I32),
+                in_=Wo_scales[:, 4 * quadrant : 4 * quadrant + 4, :].rearrange("g r n -> r g n").bitcast(I32),
+            )
+
+        bo_all = const.tile([P, CLUSTERS, E], BF16)
+        nc.scalar.dma_start(
+            out=bo_all[:].rearrange("p c e -> p (c e)"),
+            in_=bo.rearrange("c e -> (c e)").partition_broadcast(P),
+        )
+        probs_bf = const.tile([P, N_TILES * CLUSTERS], BF16)
+        nc.scalar.dma_start(out=probs_bf[:], in_=probs_rows)
+        probs = const.tile([P, N_TILES, CLUSTERS], F32)
+        nc.vector.tensor_copy(out=probs[:].rearrange("p j c -> p (j c)"), in_=probs_bf[:])
+
+        identity = const.tile([P, P], F32)
+        make_identity(nc, identity[:])
+
+        x_chunks = []
+        w_words = const.tile([P, CLUSTERS, E], U32, align_bytes=64)
+        for chunk in range(N_TILES // CHUNK):
+            x_chunk = x_pool.tile([P, HALVES, CHUNK, K], BF16)
+            nc.sync.dma_start(out=x_chunk[:], in_=x_rows[:, :, chunk * CHUNK : (chunk + 1) * CHUNK, :])
+            x_chunks.append(x_chunk)
+            if chunk == 0:
+                for c in range(CLUSTERS):
+                    nc.sync.dma_start(
+                        out=w_words[:, c, :].bitcast(I32),
+                        in_=Wo_words[c].rearrange("p n t -> p (n t)").bitcast(I32),
+                    )
+
+        grouped_of = {}
+        codes_of = {}
+        bias_of = {}
+
+        def transpose_and_regroup(j):
+            x_words = x_chunks[j // CHUNK][:].bitcast(F32)
+            xt = psum_x.tile([P, 2 * HALVES, P], F32)
+            for half in range(HALVES):
+                for u in range(2):
+                    nc.tensor.transpose(xt[:, 2 * half + u, :], x_words[:, half, j % CHUNK, u:WORDS:2], identity[:])
+            grouped = quant.tile([P, CLUSTERS, P * 4], BF16, align_bytes=64)
+            by_cluster = xt[:].rearrange("p s (b c) -> p c b s", c=CLUSTERS)
+            nc.scalar.copy(
+                out=grouped[:, 0, :].bitcast(F32).rearrange("p (b s) -> p b s", s=2 * HALVES), in_=by_cluster[:, 0]
+            )
+            nc.vector.tensor_copy(
+                out=grouped[:, 1, :].bitcast(F32).rearrange("p (b s) -> p b s", s=2 * HALVES), in_=by_cluster[:, 1]
+            )
+            grouped_of[j] = grouped
+
+        def weighted_bias(j):
+            bias0 = bias_pool.tile([P, E], F32)
+            bias1 = bias_pool.tile([P, E], F32)
+            nc.scalar.activation(out=bias0[:], in_=bo_all[:, 0, :], func=COPY, scale=probs[:, j, 0:1])
+            nc.scalar.activation(out=bias1[:], in_=bo_all[:, 1, :], func=COPY, scale=probs[:, j, 1:2])
+            bias = bias_pool.tile([P, E], F32)
+            nc.gpsimd.tensor_tensor(out=bias[:], in0=bias0[:], in1=bias1[:], op=ADD)
+            bias_of[j] = bias
+
+        def quantise(j):
+            codes = quant.tile([P, CLUSTERS, P], U32, align_bytes=64)
+            scales = quant.tile([P, CLUSTERS, P], U8, align_bytes=64)
+            nc.vector.quantize_mx(
+                out=codes[:].rearrange("p c m -> p (c m)").bitcast(FP8X4),
+                scales=scales[:].rearrange("p c m -> p (c m)"),
+                in_=grouped_of[j][:].rearrange("p c f -> p (c f)"),
+            )
+            codes_of[j] = (codes, scales)
+
+        stores = {}
+
+        def project_and_mix(j):
+            codes, scales = codes_of[j]
+            bias = bias_of[j]
+            acc = {}
+            for c in range(CLUSTERS):
+                for n in range(E_BANKS):
+                    proj = psum_acc.tile([P, BANK], F32)
+                    nc.tensor.matmul_mx(
+                        out=proj[:],
+                        lhsT=codes[:, c, :].bitcast(FP8X4),
+                        lhsT_scale=scales[:, c, :],
+                        rhs=w_words[:, c, n * BANK : (n + 1) * BANK].bitcast(FP8X4),
+                        rhs_scale=w_scales[:, c, n * BANK : (n + 1) * BANK],
+                        start=True,
+                        stop=True,
+                    )
+                    acc[(c, n)] = proj
+            if j % STORE == 0:
+                fused = result.tile([P, STORE, E], F32)
+                stores[0] = fused
+            fused = stores[0]
+            partial = result.tile([P, E], F32)
+            for n in range(E_BANKS):
+                cols = slice(n * BANK, (n + 1) * BANK)
+                nc.vector.scalar_tensor_tensor(
+                    out=partial[:, cols], in0=acc[(0, n)][:], scalar=probs[:, j, 0:1], in1=bias[:, cols], op0=MULT, op1=ADD
+                )
+            for n in range(E_BANKS):
+                cols = slice(n * BANK, (n + 1) * BANK)
+                nc.vector.scalar_tensor_tensor(
+                    out=fused[:, j % STORE, cols], in0=acc[(1, n)][:], scalar=probs[:, j, 1:2], in1=partial[:, cols], op0=MULT, op1=ADD
+                )
+            if j % STORE == STORE - 1:
+                nc.sync.dma_start(out=out_rows[:, j - STORE + 1 : j + 1, :], in_=fused[:])
+
+        for i in range(N_TILES + 2):
+            if i < N_TILES:
+                transpose_and_regroup(i)
+                weighted_bias(i)
+            if 1 <= i <= N_TILES:
+                quantise(i - 1)
+            if i >= 2:
+                project_and_mix(i - 2)

@@ -22,6 +22,9 @@ E_BANKS = E // BANK
 WORDS = K // 2
 CHUNK = 4
 STORE = 2
+ROWS = P // CLUSTERS
+E_PLAIN = 768
+E_REST = E - E_PLAIN
 
 FLOPS = 2 * BATCH * SEQ * CLUSTERS * K * E
 
@@ -39,8 +42,15 @@ def tile_model_pa_t_e_kernel(tc, attn_ctx, Wo_words, Wo_scales, bo, cluster_prob
         quant = stack.enter_context(tc.tile_pool(name="quant", bufs=3))
         bias_pool = stack.enter_context(tc.tile_pool(name="bias", bufs=4))
         result = stack.enter_context(tc.tile_pool(name="result", bufs=3))
-        psum_x = stack.enter_context(tc.psum_pool(name="psum_x", bufs=2))
-        psum_acc = stack.enter_context(tc.psum_pool(name="psum_acc", bufs=6))
+        psum_x = stack.enter_context(tc.psum_pool(name="psum_x", bufs=1))
+        psum_bias = stack.enter_context(tc.psum_pool(name="psum_bias", bufs=2))
+        psum_acc = stack.enter_context(tc.psum_pool(name="psum_acc", bufs=5))
+
+        x_chunks = []
+        for chunk in range(N_TILES // CHUNK):
+            x_chunk = x_pool.tile([P, HALVES, CHUNK, K], BF16)
+            x_chunks.append(x_chunk)
+        nc.sync.dma_start(out=x_chunks[0][:], in_=x_rows[:, :, 0:CHUNK, :])
 
         w_scales = const.tile([P, CLUSTERS, E], U8, align_bytes=64)
         nc.vector.memset(w_scales[:].bitcast(I32), 0)
@@ -49,36 +59,43 @@ def tile_model_pa_t_e_kernel(tc, attn_ctx, Wo_words, Wo_scales, bo, cluster_prob
                 out=w_scales[32 * quadrant : 32 * quadrant + 4].bitcast(I32),
                 in_=Wo_scales[:, 4 * quadrant : 4 * quadrant + 4, :].rearrange("g r n -> r g n").bitcast(I32),
             )
+        w_words = const.tile([P, CLUSTERS, E], U32, align_bytes=64)
+        for c in range(CLUSTERS):
+            nc.sync.dma_start(
+                out=w_words[:, c, :].bitcast(I32),
+                in_=Wo_words[c].rearrange("p n t -> p (n t)").bitcast(I32),
+            )
+        for chunk in range(1, N_TILES // CHUNK):
+            nc.sync.dma_start(out=x_chunks[chunk][:], in_=x_rows[:, :, chunk * CHUNK : (chunk + 1) * CHUNK, :])
 
-        bo_all = const.tile([P, CLUSTERS, E], BF16)
-        nc.scalar.dma_start(
-            out=bo_all[:].rearrange("p c e -> p (c e)"),
-            in_=bo.rearrange("c e -> (c e)").partition_broadcast(P),
-        )
-        probs_bf = const.tile([P, N_TILES * CLUSTERS], BF16)
-        nc.scalar.dma_start(out=probs_bf[:], in_=probs_rows)
-        probs = const.tile([P, N_TILES, CLUSTERS], F32)
-        nc.vector.tensor_copy(out=probs[:].rearrange("p j c -> p (j c)"), in_=probs_bf[:])
+        probs_bf = const.tile([P, N_TILES, CLUSTERS], BF16)
+        nc.scalar.dma_start(out=probs_bf[:].rearrange("p j c -> p (j c)"), in_=probs_rows)
+        bo_plain = const.tile([P, E_PLAIN], BF16)
+        bo_rest = const.tile([P, CLUSTERS, E_REST], BF16)
+        for c in range(CLUSTERS):
+            nc.scalar.dma_start(
+                out=bo_plain[c * ROWS : (c + 1) * ROWS, :], in_=bo[c, 0:E_PLAIN].partition_broadcast(ROWS)
+            )
+            nc.scalar.dma_start(out=bo_rest[:, c, :], in_=bo[c, E_PLAIN:E].partition_broadcast(P))
 
         identity = const.tile([P, P], F32)
         make_identity(nc, identity[:])
-
-        x_chunks = []
-        w_words = const.tile([P, CLUSTERS, E], U32, align_bytes=64)
-        for chunk in range(N_TILES // CHUNK):
-            x_chunk = x_pool.tile([P, HALVES, CHUNK, K], BF16)
-            nc.sync.dma_start(out=x_chunk[:], in_=x_rows[:, :, chunk * CHUNK : (chunk + 1) * CHUNK, :])
-            x_chunks.append(x_chunk)
-            if chunk == 0:
-                for c in range(CLUSTERS):
-                    nc.sync.dma_start(
-                        out=w_words[:, c, :].bitcast(I32),
-                        in_=Wo_words[c].rearrange("p n t -> p (n t)").bitcast(I32),
-                    )
+        probs = const.tile([P, CLUSTERS, ROWS], F32)
+        nc.vector.memset(probs[:], 0.0)
+        nc.vector.tensor_copy(out=probs[:, :, 0:N_TILES], in_=probs_bf[:].rearrange("p j c -> p c j"))
+        probs_t_psum = psum_bias.tile([P, BANK], F32, tag="bias_psum")
+        nc.tensor.transpose(probs_t_psum[:, 0:P], probs[:].rearrange("p c j -> p (c j)"), identity[:])
+        probs_t = const.tile([P, P], BF16)
+        nc.vector.tensor_copy(out=probs_t[:], in_=probs_t_psum[:, 0:P])
+        row_of_tile = const.tile([P, N_TILES], F32)
+        nc.vector.tensor_tensor(
+            out=row_of_tile[:], in0=identity[:, 0:N_TILES], in1=identity[:, ROWS : ROWS + N_TILES], op=ADD
+        )
 
         grouped_of = {}
         codes_of = {}
         bias_of = {}
+        fused_of = {}
 
         def transpose_and_regroup(j):
             x_words = x_chunks[j // CHUNK][:].bitcast(F32)
@@ -86,23 +103,29 @@ def tile_model_pa_t_e_kernel(tc, attn_ctx, Wo_words, Wo_scales, bo, cluster_prob
             for half in range(HALVES):
                 for u in range(2):
                     nc.tensor.transpose(xt[:, 2 * half + u, :], x_words[:, half, j % CHUNK, u:WORDS:2], identity[:])
-            grouped = quant.tile([P, CLUSTERS, P * 4], BF16, align_bytes=64)
-            by_cluster = xt[:].rearrange("p s (b c) -> p c b s", c=CLUSTERS)
+            grouped = quant.tile([P, CLUSTERS * P * 4], BF16, align_bytes=64)
             nc.scalar.copy(
-                out=grouped[:, 0, :].bitcast(F32).rearrange("p (b s) -> p b s", s=2 * HALVES), in_=by_cluster[:, 0]
-            )
-            nc.vector.tensor_copy(
-                out=grouped[:, 1, :].bitcast(F32).rearrange("p (b s) -> p b s", s=2 * HALVES), in_=by_cluster[:, 1]
+                out=grouped[:].bitcast(F32).rearrange("p (c b s) -> p c b s", c=CLUSTERS, s=2 * HALVES),
+                in_=xt[:].rearrange("p s (b c) -> p c b s", c=CLUSTERS),
             )
             grouped_of[j] = grouped
 
         def weighted_bias(j):
-            bias0 = bias_pool.tile([P, E], F32)
-            bias1 = bias_pool.tile([P, E], F32)
-            nc.scalar.activation(out=bias0[:], in_=bo_all[:, 0, :], func=COPY, scale=probs[:, j, 0:1])
-            nc.scalar.activation(out=bias1[:], in_=bo_all[:, 1, :], func=COPY, scale=probs[:, j, 1:2])
             bias = bias_pool.tile([P, E], F32)
-            nc.gpsimd.tensor_tensor(out=bias[:], in0=bias0[:], in1=bias1[:], op=ADD)
+            probs_t_j = bias_pool.tile([P, P], BF16)
+            nc.scalar.activation(out=probs_t_j[:], in_=probs_t[:], func=COPY, scale=row_of_tile[:, j : j + 1])
+            for first in range(0, E_PLAIN, BANK):
+                width = min(BANK, E_PLAIN - first)
+                bias_psum = psum_bias.tile([P, BANK], F32)
+                nc.tensor.matmul(
+                    out=bias_psum[:, 0:width], lhsT=probs_t_j[:], rhs=bo_plain[:, first : first + width], start=True, stop=True
+                )
+                nc.scalar.copy(out=bias[:, first : first + width], in_=bias_psum[:, 0:width])
+            bias0 = bias_pool.tile([P, E_REST], F32)
+            nc.scalar.activation(out=bias0[:], in_=bo_rest[:, 0, :], func=COPY, scale=probs[:, 0, j : j + 1])
+            nc.vector.scalar_tensor_tensor(
+                out=bias[:, E_PLAIN:E], in0=bo_rest[:, 1, :], scalar=probs[:, 1, j : j + 1], in1=bias0[:], op0=MULT, op1=ADD
+            )
             bias_of[j] = bias
 
         def quantise(j):
@@ -111,16 +134,14 @@ def tile_model_pa_t_e_kernel(tc, attn_ctx, Wo_words, Wo_scales, bo, cluster_prob
             nc.vector.quantize_mx(
                 out=codes[:].rearrange("p c m -> p (c m)").bitcast(FP8X4),
                 scales=scales[:].rearrange("p c m -> p (c m)"),
-                in_=grouped_of[j][:].rearrange("p c f -> p (c f)"),
+                in_=grouped_of[j][:],
             )
             codes_of[j] = (codes, scales)
-
-        stores = {}
 
         def project_and_mix(j):
             codes, scales = codes_of[j]
             bias = bias_of[j]
-            acc = {}
+            proj_of = {}
             for c in range(CLUSTERS):
                 for n in range(E_BANKS):
                     proj = psum_acc.tile([P, BANK], F32)
@@ -133,21 +154,21 @@ def tile_model_pa_t_e_kernel(tc, attn_ctx, Wo_words, Wo_scales, bo, cluster_prob
                         start=True,
                         stop=True,
                     )
-                    acc[(c, n)] = proj
+                    proj_of[(c, n)] = proj
             if j % STORE == 0:
                 fused = result.tile([P, STORE, E], F32)
-                stores[0] = fused
-            fused = stores[0]
+                fused_of[j // STORE] = fused
+            fused = fused_of[j // STORE]
             partial = result.tile([P, E], F32)
             for n in range(E_BANKS):
                 cols = slice(n * BANK, (n + 1) * BANK)
                 nc.vector.scalar_tensor_tensor(
-                    out=partial[:, cols], in0=acc[(0, n)][:], scalar=probs[:, j, 0:1], in1=bias[:, cols], op0=MULT, op1=ADD
+                    out=partial[:, cols], in0=proj_of[(0, n)][:], scalar=probs[:, 0, j : j + 1], in1=bias[:, cols], op0=MULT, op1=ADD
                 )
             for n in range(E_BANKS):
                 cols = slice(n * BANK, (n + 1) * BANK)
                 nc.vector.scalar_tensor_tensor(
-                    out=fused[:, j % STORE, cols], in0=acc[(1, n)][:], scalar=probs[:, j, 1:2], in1=partial[:, cols], op0=MULT, op1=ADD
+                    out=fused[:, j % STORE, cols], in0=proj_of[(1, n)][:], scalar=probs[:, 1, j : j + 1], in1=partial[:, cols], op0=MULT, op1=ADD
                 )
             if j % STORE == STORE - 1:
                 nc.sync.dma_start(out=out_rows[:, j - STORE + 1 : j + 1, :], in_=fused[:])

@@ -122,10 +122,10 @@ def tile_model_pa_t_e_kernel(tc, attn_ctx, Wo_words, Wo_scales, bo, cluster_prob
                 )
                 nc.scalar.copy(out=bias[:, first : first + width], in_=bias_psum[:, 0:width])
             bias0 = bias_pool.tile([P, E_REST], F32)
+            bias1 = bias_pool.tile([P, E_REST], F32)
             nc.scalar.activation(out=bias0[:], in_=bo_rest[:, 0, :], func=COPY, scale=probs[:, 0, j : j + 1])
-            nc.vector.scalar_tensor_tensor(
-                out=bias[:, E_PLAIN:E], in0=bo_rest[:, 1, :], scalar=probs[:, 1, j : j + 1], in1=bias0[:], op0=MULT, op1=ADD
-            )
+            nc.scalar.activation(out=bias1[:], in_=bo_rest[:, 1, :], func=COPY, scale=probs[:, 1, j : j + 1])
+            nc.gpsimd.tensor_tensor(out=bias[:, E_PLAIN:E], in0=bias0[:], in1=bias1[:], op=ADD)
             bias_of[j] = bias
 
         def quantise(j):

@@ -92,17 +92,26 @@ def tile_model_pa_t_e_kernel(tc, attn_ctx, Wo_words, Wo_scales, bo, cluster_prob
             out=row_of_tile[:], in0=identity[:, 0:N_TILES], in1=identity[:, ROWS : ROWS + N_TILES], op=ADD
         )
 
+        xt_of = {}
+        masked_of = {}
+        bias_psum_of = {}
+        proj_of = {}
+        partial_of = {}
         grouped_of = {}
         codes_of = {}
         bias_of = {}
         fused_of = {}
 
-        def transpose_and_regroup(j):
+        def transpose(j):
             x_words = x_chunks[j // CHUNK][:].bitcast(F32)
             xt = psum_x.tile([P, 2 * HALVES, P], F32)
             for half in range(HALVES):
                 for u in range(2):
                     nc.tensor.transpose(xt[:, 2 * half + u, :], x_words[:, half, j % CHUNK, u:WORDS:2], identity[:])
+            xt_of[j] = xt
+
+        def regroup(j):
+            xt = xt_of[j]
             grouped = quant.tile([P, CLUSTERS * P * 4], BF16, align_bytes=64)
             nc.scalar.copy(
                 out=grouped[:].bitcast(F32).rearrange("p (c b s) -> p c b s", c=CLUSTERS, s=2 * HALVES),
@@ -110,23 +119,34 @@ def tile_model_pa_t_e_kernel(tc, attn_ctx, Wo_words, Wo_scales, bo, cluster_prob
             )
             grouped_of[j] = grouped
 
-        def weighted_bias(j):
-            bias = bias_pool.tile([P, E], F32)
+        def mask_rows(j):
             probs_t_j = bias_pool.tile([P, P], BF16)
             nc.scalar.activation(out=probs_t_j[:], in_=probs_t[:], func=COPY, scale=row_of_tile[:, j : j + 1])
+            masked_of[j] = probs_t_j
+
+        def bias_product(j):
+            banks = []
             for first in range(0, E_PLAIN, BANK):
                 width = min(BANK, E_PLAIN - first)
                 bias_psum = psum_bias.tile([P, BANK], F32)
                 nc.tensor.matmul(
-                    out=bias_psum[:, 0:width], lhsT=probs_t_j[:], rhs=bo_plain[:, first : first + width], start=True, stop=True
+                    out=bias_psum[:, 0:width], lhsT=masked_of[j][:], rhs=bo_plain[:, first : first + width], start=True, stop=True
                 )
+                banks.append((first, width, bias_psum))
+            bias_psum_of[j] = banks
+
+        def bias_out(j):
+            bias = bias_pool.tile([P, E], F32)
+            for first, width, bias_psum in bias_psum_of[j]:
                 nc.scalar.copy(out=bias[:, first : first + width], in_=bias_psum[:, 0:width])
+            bias_of[j] = bias
+
+        def bias_rest(j):
             bias0 = bias_pool.tile([P, E_REST], F32)
             bias1 = bias_pool.tile([P, E_REST], F32)
             nc.scalar.activation(out=bias0[:], in_=bo_rest[:, 0, :], func=COPY, scale=probs[:, 0, j : j + 1])
             nc.scalar.activation(out=bias1[:], in_=bo_rest[:, 1, :], func=COPY, scale=probs[:, 1, j : j + 1])
-            nc.gpsimd.tensor_tensor(out=bias[:, E_PLAIN:E], in0=bias0[:], in1=bias1[:], op=ADD)
-            bias_of[j] = bias
+            nc.gpsimd.tensor_tensor(out=bias_of[j][:, E_PLAIN:E], in0=bias0[:], in1=bias1[:], op=ADD)
 
         def quantise(j):
             codes = quant.tile([P, CLUSTERS, P], U32, align_bytes=64)
@@ -138,46 +158,66 @@ def tile_model_pa_t_e_kernel(tc, attn_ctx, Wo_words, Wo_scales, bo, cluster_prob
             )
             codes_of[j] = (codes, scales)
 
-        def project_and_mix(j):
+        def project(j, c):
             codes, scales = codes_of[j]
-            bias = bias_of[j]
-            proj_of = {}
-            for c in range(CLUSTERS):
-                for n in range(E_BANKS):
-                    proj = psum_acc.tile([P, BANK], F32)
-                    nc.tensor.matmul_mx(
-                        out=proj[:],
-                        lhsT=codes[:, c, :].bitcast(FP8X4),
-                        lhsT_scale=scales[:, c, :],
-                        rhs=w_words[:, c, n * BANK : (n + 1) * BANK].bitcast(FP8X4),
-                        rhs_scale=w_scales[:, c, n * BANK : (n + 1) * BANK],
-                        start=True,
-                        stop=True,
-                    )
-                    proj_of[(c, n)] = proj
+            for n in range(E_BANKS):
+                proj = psum_acc.tile([P, BANK], F32)
+                nc.tensor.matmul_mx(
+                    out=proj[:],
+                    lhsT=codes[:, c, :].bitcast(FP8X4),
+                    lhsT_scale=scales[:, c, :],
+                    rhs=w_words[:, c, n * BANK : (n + 1) * BANK].bitcast(FP8X4),
+                    rhs_scale=w_scales[:, c, n * BANK : (n + 1) * BANK],
+                    start=True,
+                    stop=True,
+                )
+                proj_of[(j, c, n)] = proj
+
+        def mix_first(j):
+            partial = result.tile([P, E], F32)
+            partial_of[j] = partial
+            for n in range(E_BANKS):
+                cols = slice(n * BANK, (n + 1) * BANK)
+                nc.vector.scalar_tensor_tensor(
+                    out=partial[:, cols], in0=proj_of[(j, 0, n)][:], scalar=probs[:, 0, j : j + 1], in1=bias_of[j][:, cols], op0=MULT, op1=ADD
+                )
+
+        def mix_second(j):
             if j % STORE == 0:
                 fused = result.tile([P, STORE, E], F32)
                 fused_of[j // STORE] = fused
             fused = fused_of[j // STORE]
-            partial = result.tile([P, E], F32)
             for n in range(E_BANKS):
                 cols = slice(n * BANK, (n + 1) * BANK)
                 nc.vector.scalar_tensor_tensor(
-                    out=partial[:, cols], in0=proj_of[(0, n)][:], scalar=probs[:, 0, j : j + 1], in1=bias[:, cols], op0=MULT, op1=ADD
-                )
-            for n in range(E_BANKS):
-                cols = slice(n * BANK, (n + 1) * BANK)
-                nc.vector.scalar_tensor_tensor(
-                    out=fused[:, j % STORE, cols], in0=proj_of[(1, n)][:], scalar=probs[:, 1, j : j + 1], in1=partial[:, cols], op0=MULT, op1=ADD
+                    out=fused[:, j % STORE, cols], in0=proj_of[(j, 1, n)][:], scalar=probs[:, 1, j : j + 1], in1=partial_of[j][:, cols], op0=MULT, op1=ADD
                 )
             if j % STORE == STORE - 1:
                 nc.sync.dma_start(out=out_rows[:, j - STORE + 1 : j + 1, :], in_=fused[:])
 
-        for i in range(N_TILES + 2):
-            if i < N_TILES:
-                transpose_and_regroup(i)
-                weighted_bias(i)
-            if 1 <= i <= N_TILES:
-                quantise(i - 1)
-            if i >= 2:
-                project_and_mix(i - 2)
+        def live(j):
+            return 0 <= j < N_TILES
+
+        with tc.manual_schedule():
+            for i in range(-3, N_TILES):
+                if live(i):
+                    project(i, 0)
+                if live(i + 1):
+                    bias_out(i + 1)
+                if live(i):
+                    mix_first(i)
+                if live(i + 2):
+                    transpose(i + 2)
+                if live(i + 1):
+                    bias_rest(i + 1)
+                    quantise(i + 1)
+                if live(i):
+                    project(i, 1)
+                if live(i + 2):
+                    regroup(i + 2)
+                if live(i):
+                    mix_second(i)
+                if live(i + 3):
+                    mask_rows(i + 3)
+                if live(i + 2):
+                    bias_product(i + 2)

@@ -21,7 +21,8 @@ BANK = 512
 E_BANKS = E // BANK
 WORDS = K // 2
 CHUNK = 4
-STORE = 2
+PAIR = 2
+N_ROUNDS = N_TILES // PAIR
 ROWS = P // CLUSTERS
 E_PLAIN = 768
 E_REST = E - E_PLAIN
@@ -42,9 +43,9 @@ def tile_model_pa_t_e_kernel(tc, attn_ctx, Wo_words, Wo_scales, bo, cluster_prob
         quant = stack.enter_context(tc.tile_pool(name="quant", bufs=3))
         bias_pool = stack.enter_context(tc.tile_pool(name="bias", bufs=4))
         result = stack.enter_context(tc.tile_pool(name="result", bufs=3))
-        psum_x = stack.enter_context(tc.psum_pool(name="psum_x", bufs=1))
+        psum_x = stack.enter_context(tc.psum_pool(name="psum_x", bufs=2))
         psum_bias = stack.enter_context(tc.psum_pool(name="psum_bias", bufs=2))
-        psum_acc = stack.enter_context(tc.psum_pool(name="psum_acc", bufs=5))
+        psum_acc = stack.enter_context(tc.psum_pool(name="psum_acc", bufs=4))
 
         x_chunks = []
         for chunk in range(N_TILES // CHUNK):
@@ -111,13 +112,14 @@ def tile_model_pa_t_e_kernel(tc, attn_ctx, Wo_words, Wo_scales, bo, cluster_prob
             xt_of[j] = xt
 
         def regroup(j):
-            xt = xt_of[j]
-            grouped = quant.tile([P, CLUSTERS * P * 4], BF16, align_bytes=64)
+            if j % PAIR == 0:
+                grouped = quant.tile([P, PAIR, CLUSTERS * P * 4], BF16, align_bytes=64)
+                grouped_of[j // PAIR] = grouped
+            grouped = grouped_of[j // PAIR]
             nc.scalar.copy(
-                out=grouped[:].bitcast(F32).rearrange("p (c b s) -> p c b s", c=CLUSTERS, s=2 * HALVES),
-                in_=xt[:].rearrange("p s (b c) -> p c b s", c=CLUSTERS),
+                out=grouped[:, j % PAIR, :].bitcast(F32).rearrange("p (c b s) -> p c b s", c=CLUSTERS, s=2 * HALVES),
+                in_=xt_of[j][:].rearrange("p s (b c) -> p c b s", c=CLUSTERS),
             )
-            grouped_of[j] = grouped
 
         def mask_rows(j):
             probs_t_j = bias_pool.tile([P, P], BF16)
@@ -136,42 +138,48 @@ def tile_model_pa_t_e_kernel(tc, attn_ctx, Wo_words, Wo_scales, bo, cluster_prob
             bias_psum_of[j] = banks
 
         def bias_out(j):
-            bias = bias_pool.tile([P, E], F32)
             for first, width, bias_psum in bias_psum_of[j]:
-                nc.scalar.copy(out=bias[:, first : first + width], in_=bias_psum[:, 0:width])
-            bias_of[j] = bias
+                nc.scalar.copy(out=bias_of[j // PAIR][:, j % PAIR, first : first + width], in_=bias_psum[:, 0:width])
 
-        def bias_rest(j):
-            bias0 = bias_pool.tile([P, E_REST], F32)
-            bias1 = bias_pool.tile([P, E_REST], F32)
-            nc.scalar.activation(out=bias0[:], in_=bo_rest[:, 0, :], func=COPY, scale=probs[:, 0, j : j + 1])
-            nc.scalar.activation(out=bias1[:], in_=bo_rest[:, 1, :], func=COPY, scale=probs[:, 1, j : j + 1])
-            nc.gpsimd.tensor_tensor(out=bias_of[j][:, E_PLAIN:E], in0=bias0[:], in1=bias1[:], op=ADD)
+        def bias_rest(r):
+            bias = bias_pool.tile([P, PAIR, E], F32)
+            bias_of[r] = bias
+            bias0 = bias_pool.tile([P, PAIR, E_REST], F32)
+            bias1 = bias_pool.tile([P, PAIR, E_REST], F32)
+            for t in range(PAIR):
+                j = PAIR * r + t
+                nc.scalar.activation(out=bias0[:, t, :], in_=bo_rest[:, 0, :], func=COPY, scale=probs[:, 0, j : j + 1])
+                nc.scalar.activation(out=bias1[:, t, :], in_=bo_rest[:, 1, :], func=COPY, scale=probs[:, 1, j : j + 1])
+            nc.gpsimd.tensor_tensor(out=bias[:, :, E_PLAIN:E], in0=bias0[:], in1=bias1[:], op=ADD)
 
-        def quantise(j):
-            codes = quant.tile([P, CLUSTERS, P], U32, align_bytes=64)
-            scales = quant.tile([P, CLUSTERS, P], U8, align_bytes=64)
-            nc.vector.quantize_mx(
-                out=codes[:].rearrange("p c m -> p (c m)").bitcast(FP8X4),
-                scales=scales[:].rearrange("p c m -> p (c m)"),
-                in_=grouped_of[j][:],
-            )
-            codes_of[j] = (codes, scales)
-
-        def project(j, c):
-            codes, scales = codes_of[j]
-            for n in range(E_BANKS):
-                proj = psum_acc.tile([P, BANK], F32)
-                nc.tensor.matmul_mx(
-                    out=proj[:],
-                    lhsT=codes[:, c, :].bitcast(FP8X4),
-                    lhsT_scale=scales[:, c, :],
-                    rhs=w_words[:, c, n * BANK : (n + 1) * BANK].bitcast(FP8X4),
-                    rhs_scale=w_scales[:, c, n * BANK : (n + 1) * BANK],
-                    start=True,
-                    stop=True,
+        def quantise(r, pieces):
+            codes = quant.tile([P, PAIR * CLUSTERS, P], U32, align_bytes=64)
+            scales = quant.tile([P, PAIR * CLUSTERS, P], U8, align_bytes=64)
+            codes_of[r] = (codes, scales)
+            share = PAIR * CLUSTERS // pieces
+            for piece in range(pieces):
+                nc.vector.quantize_mx(
+                    out=codes[:, piece * share : (piece + 1) * share, :].rearrange("p c m -> p (c m)").bitcast(FP8X4),
+                    scales=scales[:, piece * share : (piece + 1) * share, :].rearrange("p c m -> p (c m)"),
+                    in_=grouped_of[r][:, piece * PAIR // pieces : (piece + 1) * PAIR // pieces, :].rearrange("p t k -> p (t k)"),
                 )
-                proj_of[(j, c, n)] = proj
+
+        def project(j):
+            codes, scales = codes_of[j // PAIR]
+            for c in range(CLUSTERS):
+                slot = (j % PAIR) * CLUSTERS + c
+                for n in range(E_BANKS):
+                    proj = psum_acc.tile([P, BANK], F32)
+                    nc.tensor.matmul_mx(
+                        out=proj[:],
+                        lhsT=codes[:, slot, :].bitcast(FP8X4),
+                        lhsT_scale=scales[:, slot, :],
+                        rhs=w_words[:, c, n * BANK : (n + 1) * BANK].bitcast(FP8X4),
+                        rhs_scale=w_scales[:, c, n * BANK : (n + 1) * BANK],
+                        start=True,
+                        stop=True,
+                    )
+                    proj_of[(j, c, n)] = proj
 
         def mix_first(j):
             partial = result.tile([P, E], F32)
@@ -179,45 +187,59 @@ def tile_model_pa_t_e_kernel(tc, attn_ctx, Wo_words, Wo_scales, bo, cluster_prob
             for n in range(E_BANKS):
                 cols = slice(n * BANK, (n + 1) * BANK)
                 nc.vector.scalar_tensor_tensor(
-                    out=partial[:, cols], in0=proj_of[(j, 0, n)][:], scalar=probs[:, 0, j : j + 1], in1=bias_of[j][:, cols], op0=MULT, op1=ADD
+                    out=partial[:, cols], in0=proj_of[(j, 0, n)][:], scalar=probs[:, 0, j : j + 1],
+                    in1=bias_of[j // PAIR][:, j % PAIR, cols], op0=MULT, op1=ADD,
                 )
 
         def mix_second(j):
-            if j % STORE == 0:
-                fused = result.tile([P, STORE, E], F32)
-                fused_of[j // STORE] = fused
-            fused = fused_of[j // STORE]
+            if j % PAIR == 0:
+                fused = result.tile([P, PAIR, E], F32)
+                fused_of[j // PAIR] = fused
+            fused = fused_of[j // PAIR]
             for n in range(E_BANKS):
                 cols = slice(n * BANK, (n + 1) * BANK)
                 nc.vector.scalar_tensor_tensor(
-                    out=fused[:, j % STORE, cols], in0=proj_of[(j, 1, n)][:], scalar=probs[:, 1, j : j + 1], in1=partial_of[j][:, cols], op0=MULT, op1=ADD
+                    out=fused[:, j % PAIR, cols], in0=proj_of[(j, 1, n)][:], scalar=probs[:, 1, j : j + 1],
+                    in1=partial_of[j][:, cols], op0=MULT, op1=ADD,
                 )
-            if j % STORE == STORE - 1:
-                nc.sync.dma_start(out=out_rows[:, j - STORE + 1 : j + 1, :], in_=fused[:])
+            if j % PAIR == PAIR - 1:
+                nc.sync.dma_start(out=out_rows[:, j - PAIR + 1 : j + 1, :], in_=fused[:])
 
         def live(j):
             return 0 <= j < N_TILES
 
         with tc.manual_schedule():
-            for i in range(-3, N_TILES):
-                if live(i):
-                    project(i, 0)
-                if live(i + 1):
-                    bias_out(i + 1)
-                if live(i):
-                    mix_first(i)
-                if live(i + 2):
-                    transpose(i + 2)
-                if live(i + 1):
-                    bias_rest(i + 1)
-                    quantise(i + 1)
-                if live(i):
-                    project(i, 1)
-                if live(i + 2):
-                    regroup(i + 2)
-                if live(i):
-                    mix_second(i)
-                if live(i + 3):
-                    mask_rows(i + 3)
-                if live(i + 2):
-                    bias_product(i + 2)
+            for r in range(-2, N_ROUNDS):
+                a = PAIR * r
+                b = a + 1
+                if live(a):
+                    project(a)
+                if r == 0:
+                    bias_product(b)
+                    bias_out(b)
+                if live(a + 2):
+                    bias_rest(r + 1)
+                if live(a):
+                    mix_first(a)
+                    mix_second(a)
+                if live(a + 2):
+                    transpose(a + 2)
+                    transpose(b + 2)
+                    regroup(a + 2)
+                    regroup(b + 2)
+                if live(a + 4):
+                    mask_rows(a + 4)
+                    mask_rows(b + 4)
+                if live(a + 2):
+                    bias_product(a + 2)
+                    bias_out(a + 2)
+                if live(b):
+                    project(b)
+                    mix_first(b)
+                if live(a + 2):
+                    quantise(r + 1, PAIR if r < 0 else 1)
+                if live(b):
+                    mix_second(b)
+                if live(b + 2) and r >= 0:
+                    bias_product(b + 2)
+                    bias_out(b + 2)

@@ -20,7 +20,7 @@ N_TILES = SEQ // HALVES
 BANK = 512
 E_BANKS = E // BANK
 WORDS = K // 2
-CHUNK = 4
+X_LOADS = (1, 1, 2) + (4,) * 7
 PAIR = 2
 N_ROUNDS = N_TILES // PAIR
 ROWS = P // CLUSTERS
@@ -39,7 +39,7 @@ def tile_model_pa_t_e_kernel(tc, attn_ctx, Wo_words, Wo_scales, bo, cluster_prob
 
     with ExitStack() as stack:
         const = stack.enter_context(tc.tile_pool(name="const", bufs=1))
-        x_pool = stack.enter_context(tc.tile_pool(name="x", bufs=N_TILES // CHUNK))
+        x_pool = stack.enter_context(tc.tile_pool(name="x", bufs=1))
         quant = stack.enter_context(tc.tile_pool(name="quant", bufs=3))
         bias_pool = stack.enter_context(tc.tile_pool(name="bias", bufs=4))
         result = stack.enter_context(tc.tile_pool(name="result", bufs=3))
@@ -47,27 +47,36 @@ def tile_model_pa_t_e_kernel(tc, attn_ctx, Wo_words, Wo_scales, bo, cluster_prob
         psum_bias = stack.enter_context(tc.psum_pool(name="psum_bias", bufs=2))
         psum_acc = stack.enter_context(tc.psum_pool(name="psum_acc", bufs=4))
 
-        x_chunks = []
-        for chunk in range(N_TILES // CHUNK):
-            x_chunk = x_pool.tile([P, HALVES, CHUNK, K], BF16)
-            x_chunks.append(x_chunk)
-        nc.sync.dma_start(out=x_chunks[0][:], in_=x_rows[:, :, 0:CHUNK, :])
+        x_of = {}
+
+        def load_x(first, count):
+            x_chunk = x_pool.tile([P, HALVES, count, K], BF16, name="x%d" % first)
+            nc.sync.dma_start(out=x_chunk[:], in_=x_rows[:, :, first : first + count, :])
+            for place in range(count):
+                x_of[first + place] = (x_chunk, place)
 
         w_scales = const.tile([P, CLUSTERS, E], U8, align_bytes=64)
         nc.vector.memset(w_scales[:].bitcast(I32), 0)
-        for quadrant in range(4):
-            nc.sync.dma_start(
-                out=w_scales[32 * quadrant : 32 * quadrant + 4].bitcast(I32),
-                in_=Wo_scales[:, 4 * quadrant : 4 * quadrant + 4, :].rearrange("g r n -> r g n").bitcast(I32),
-            )
         w_words = const.tile([P, CLUSTERS, E], U32, align_bytes=64)
-        for c in range(CLUSTERS):
+
+        def load_w(c):
             nc.sync.dma_start(
                 out=w_words[:, c, :].bitcast(I32),
                 in_=Wo_words[c].rearrange("p n t -> p (n t)").bitcast(I32),
             )
-        for chunk in range(1, N_TILES // CHUNK):
-            nc.sync.dma_start(out=x_chunks[chunk][:], in_=x_rows[:, :, chunk * CHUNK : (chunk + 1) * CHUNK, :])
+
+        first = 0
+        for number, count in enumerate(X_LOADS):
+            load_x(first, count)
+            first += count
+            if number == 0:
+                for quadrant in range(4):
+                    nc.sync.dma_start(
+                        out=w_scales[32 * quadrant : 32 * quadrant + 4].bitcast(I32),
+                        in_=Wo_scales[:, 4 * quadrant : 4 * quadrant + 4, :].rearrange("g r n -> r g n").bitcast(I32),
+                    )
+            if number < CLUSTERS:
+                load_w(number)
 
         probs_bf = const.tile([P, N_TILES, CLUSTERS], BF16)
         nc.scalar.dma_start(out=probs_bf[:].rearrange("p j c -> p (j c)"), in_=probs_rows)
@@ -78,6 +87,10 @@ def tile_model_pa_t_e_kernel(tc, attn_ctx, Wo_words, Wo_scales, bo, cluster_prob
                 out=bo_plain[c * ROWS : (c + 1) * ROWS, :], in_=bo[c, 0:E_PLAIN].partition_broadcast(ROWS)
             )
             nc.scalar.dma_start(out=bo_rest[:, c, :], in_=bo[c, E_PLAIN:E].partition_broadcast(P))
+
+        warm = const.tile([P, 2], F32)
+        nc.vector.memset(warm[:], 0.0)
+        nc.scalar.activation(out=warm[:, 1:2], in_=warm[:, 0:1], func=COPY)
 
         identity = const.tile([P, P], F32)
         make_identity(nc, identity[:])
@@ -101,14 +114,16 @@ def tile_model_pa_t_e_kernel(tc, attn_ctx, Wo_words, Wo_scales, bo, cluster_prob
         grouped_of = {}
         codes_of = {}
         bias_of = {}
+        terms_of = {}
         fused_of = {}
 
         def transpose(j):
-            x_words = x_chunks[j // CHUNK][:].bitcast(F32)
+            x_chunk, place = x_of[j]
+            x_words = x_chunk[:].bitcast(F32)
             xt = psum_x.tile([P, 2 * HALVES, P], F32)
             for half in range(HALVES):
                 for u in range(2):
-                    nc.tensor.transpose(xt[:, 2 * half + u, :], x_words[:, half, j % CHUNK, u:WORDS:2], identity[:])
+                    nc.tensor.transpose(xt[:, 2 * half + u, :], x_words[:, half, place, u:WORDS:2], identity[:])
             xt_of[j] = xt
 
         def regroup(j):
@@ -141,28 +156,33 @@ def tile_model_pa_t_e_kernel(tc, attn_ctx, Wo_words, Wo_scales, bo, cluster_prob
             for first, width, bias_psum in bias_psum_of[j]:
                 nc.scalar.copy(out=bias_of[j // PAIR][:, j % PAIR, first : first + width], in_=bias_psum[:, 0:width])
 
-        def bias_rest(r):
-            bias = bias_pool.tile([P, PAIR, E], F32)
-            bias_of[r] = bias
-            bias0 = bias_pool.tile([P, PAIR, E_REST], F32)
-            bias1 = bias_pool.tile([P, PAIR, E_REST], F32)
-            for t in range(PAIR):
+        def bias_rest(r, tiles):
+            if r not in bias_of:
+                bias = bias_pool.tile([P, PAIR, E], F32)
+                bias0 = bias_pool.tile([P, PAIR, E_REST], F32)
+                bias1 = bias_pool.tile([P, PAIR, E_REST], F32)
+                bias_of[r] = bias
+                terms_of[r] = (bias0, bias1)
+            bias0, bias1 = terms_of[r]
+            for t in tiles:
                 j = PAIR * r + t
                 nc.scalar.activation(out=bias0[:, t, :], in_=bo_rest[:, 0, :], func=COPY, scale=probs[:, 0, j : j + 1])
                 nc.scalar.activation(out=bias1[:, t, :], in_=bo_rest[:, 1, :], func=COPY, scale=probs[:, 1, j : j + 1])
-            nc.gpsimd.tensor_tensor(out=bias[:, :, E_PLAIN:E], in0=bias0[:], in1=bias1[:], op=ADD)
+            span = slice(tiles[0], tiles[-1] + 1)
+            nc.gpsimd.tensor_tensor(out=bias_of[r][:, span, E_PLAIN:E], in0=bias0[:, span, :], in1=bias1[:, span, :], op=ADD)
 
-        def quantise(r, pieces):
-            codes = quant.tile([P, PAIR * CLUSTERS, P], U32, align_bytes=64)
-            scales = quant.tile([P, PAIR * CLUSTERS, P], U8, align_bytes=64)
-            codes_of[r] = (codes, scales)
-            share = PAIR * CLUSTERS // pieces
-            for piece in range(pieces):
-                nc.vector.quantize_mx(
-                    out=codes[:, piece * share : (piece + 1) * share, :].rearrange("p c m -> p (c m)").bitcast(FP8X4),
-                    scales=scales[:, piece * share : (piece + 1) * share, :].rearrange("p c m -> p (c m)"),
-                    in_=grouped_of[r][:, piece * PAIR // pieces : (piece + 1) * PAIR // pieces, :].rearrange("p t k -> p (t k)"),
-                )
+        def quantise(r, tiles):
+            if r not in codes_of:
+                codes = quant.tile([P, PAIR * CLUSTERS, P], U32, align_bytes=64)
+                scales = quant.tile([P, PAIR * CLUSTERS, P], U8, align_bytes=64)
+                codes_of[r] = (codes, scales)
+            codes, scales = codes_of[r]
+            slots = slice(tiles[0] * CLUSTERS, (tiles[-1] + 1) * CLUSTERS)
+            nc.vector.quantize_mx(
+                out=codes[:, slots, :].rearrange("p c m -> p (c m)").bitcast(FP8X4),
+                scales=scales[:, slots, :].rearrange("p c m -> p (c m)"),
+                in_=grouped_of[r][:, tiles[0] : tiles[-1] + 1, :].rearrange("p t k -> p (t k)"),
+            )
 
         def project(j):
             codes, scales = codes_of[j // PAIR]
@@ -202,26 +222,44 @@ def tile_model_pa_t_e_kernel(tc, attn_ctx, Wo_words, Wo_scales, bo, cluster_prob
                     out=fused[:, j % PAIR, cols], in0=proj_of[(j, 1, n)][:], scalar=probs[:, 1, j : j + 1],
                     in1=partial_of[j][:, cols], op0=MULT, op1=ADD,
                 )
-            if j % PAIR == PAIR - 1:
+                if j == N_TILES - 1:
+                    nc.sync.dma_start(out=out_rows[:, j, cols], in_=fused[:, j % PAIR, cols])
+            if j == N_TILES - PAIR:
+                nc.sync.dma_start(out=out_rows[:, j, :], in_=fused[:, j % PAIR, :])
+            elif j % PAIR == PAIR - 1 and j < N_TILES - 1:
                 nc.sync.dma_start(out=out_rows[:, j - PAIR + 1 : j + 1, :], in_=fused[:])
 
         def live(j):
             return 0 <= j < N_TILES
 
+        both = (0, 1)
         with tc.manual_schedule():
-            for r in range(-2, N_ROUNDS):
+            mask_rows(0)
+            transpose(0)
+            regroup(0)
+            quantise(0, (0,))
+            bias_rest(0, (0,))
+            bias_product(0)
+            bias_out(0)
+            mask_rows(1)
+            transpose(1)
+            regroup(1)
+            bias_rest(0, (1,))
+            mask_rows(2)
+            mask_rows(3)
+            for r in range(N_ROUNDS):
                 a = PAIR * r
                 b = a + 1
-                if live(a):
-                    project(a)
+                project(a)
                 if r == 0:
                     bias_product(b)
                     bias_out(b)
                 if live(a + 2):
-                    bias_rest(r + 1)
-                if live(a):
-                    mix_first(a)
-                    mix_second(a)
+                    bias_rest(r + 1, both)
+                mix_first(a)
+                if r == 0:
+                    quantise(0, (1,))
+                mix_second(a)
                 if live(a + 2):
                     transpose(a + 2)
                     transpose(b + 2)
@@ -233,13 +271,11 @@ def tile_model_pa_t_e_kernel(tc, attn_ctx, Wo_words, Wo_scales, bo, cluster_prob
                 if live(a + 2):
                     bias_product(a + 2)
                     bias_out(a + 2)
-                if live(b):
-                    project(b)
-                    mix_first(b)
+                project(b)
+                mix_first(b)
                 if live(a + 2):
-                    quantise(r + 1, PAIR if r < 0 else 1)
-                if live(b):
-                    mix_second(b)
-                if live(b + 2) and r >= 0:
+                    quantise(r + 1, both)
+                mix_second(b)
+                if live(b + 2):
                     bias_product(b + 2)
                     bias_out(b + 2)

@@ -12,6 +12,7 @@ FP8X4 = mybir.dt.float8_e4m3fn_x4
 MULT = mybir.AluOpType.mult
 ADD = mybir.AluOpType.add
 COPY = mybir.ActivationFunctionType.Copy
+AXIS_X = mybir.AxisListType.X
 
 P = 128
 BATCH, SEQ, CLUSTERS, K, E = 64, 64, 2, 512, 1024
@@ -23,6 +24,7 @@ WORDS = K // 2
 X_LOADS = (1, 1, 2) + (4,) * 7
 PAIR = 2
 N_ROUNDS = N_TILES // PAIR
+GROUP = 4
 ROWS = P // CLUSTERS
 E_PLAIN = 768
 E_REST = E - E_PLAIN
@@ -105,6 +107,13 @@ def tile_model_pa_t_e_kernel(tc, attn_ctx, Wo_words, Wo_scales, bo, cluster_prob
         nc.vector.tensor_tensor(
             out=row_of_tile[:], in0=identity[:, 0:N_TILES], in1=identity[:, ROWS : ROWS + N_TILES], op=ADD
         )
+        rows_of_group = const.tile([P, N_TILES // GROUP], F32)
+        nc.vector.tensor_reduce(out=rows_of_group[:], in_=row_of_tile[:].rearrange("p (g t) -> p g t", t=GROUP), axis=AXIS_X, op=ADD)
+        rows_of_place = const.tile([P, GROUP], F32)
+        nc.vector.tensor_reduce(out=rows_of_place[:], in_=row_of_tile[:].rearrange("p (g t) -> p t g", t=GROUP), axis=AXIS_X, op=ADD)
+        bo_place = const.tile([P, GROUP, E_PLAIN], BF16)
+        for t in range(GROUP):
+            nc.vector.tensor_scalar_mul(out=bo_place[:, t, :], in0=bo_plain[:], scalar1=rows_of_place[:, t : t + 1])
 
         xt_of = {}
         masked_of = {}
@@ -136,10 +145,10 @@ def tile_model_pa_t_e_kernel(tc, attn_ctx, Wo_words, Wo_scales, bo, cluster_prob
                 in_=xt_of[j][:].rearrange("p s (b c) -> p c b s", c=CLUSTERS),
             )
 
-        def mask_rows(j):
-            probs_t_j = bias_pool.tile([P, P], BF16)
-            nc.scalar.activation(out=probs_t_j[:], in_=probs_t[:], func=COPY, scale=row_of_tile[:, j : j + 1])
-            masked_of[j] = probs_t_j
+        def mask_rows(g):
+            probs_t_g = bias_pool.tile([P, P], BF16)
+            nc.scalar.activation(out=probs_t_g[:], in_=probs_t[:], func=COPY, scale=rows_of_group[:, g : g + 1])
+            masked_of[g] = probs_t_g
 
         def bias_product(j):
             banks = []
@@ -147,7 +156,7 @@ def tile_model_pa_t_e_kernel(tc, attn_ctx, Wo_words, Wo_scales, bo, cluster_prob
                 width = min(BANK, E_PLAIN - first)
                 bias_psum = psum_bias.tile([P, BANK], F32)
                 nc.tensor.matmul(
-                    out=bias_psum[:, 0:width], lhsT=masked_of[j][:], rhs=bo_plain[:, first : first + width], start=True, stop=True
+                    out=bias_psum[:, 0:width], lhsT=masked_of[j // GROUP][:], rhs=bo_place[:, j % GROUP, first : first + width], start=True, stop=True
                 )
                 banks.append((first, width, bias_psum))
             bias_psum_of[j] = banks
@@ -184,9 +193,9 @@ def tile_model_pa_t_e_kernel(tc, attn_ctx, Wo_words, Wo_scales, bo, cluster_prob
                 in_=grouped_of[r][:, tiles[0] : tiles[-1] + 1, :].rearrange("p t k -> p (t k)"),
             )
 
-        def project(j):
+        def project(j, clusters):
             codes, scales = codes_of[j // PAIR]
-            for c in range(CLUSTERS):
+            for c in clusters:
                 slot = (j % PAIR) * CLUSTERS + c
                 for n in range(E_BANKS):
                     proj = psum_acc.tile([P, BANK], F32)
@@ -241,41 +250,46 @@ def tile_model_pa_t_e_kernel(tc, attn_ctx, Wo_words, Wo_scales, bo, cluster_prob
             bias_rest(0, (0,))
             bias_product(0)
             bias_out(0)
-            mask_rows(1)
             transpose(1)
             regroup(1)
             bias_rest(0, (1,))
-            mask_rows(2)
-            mask_rows(3)
             for r in range(N_ROUNDS):
                 a = PAIR * r
                 b = a + 1
-                project(a)
+                project(a, both)
                 if r == 0:
                     bias_product(b)
-                    bias_out(b)
                 if live(a + 2):
-                    bias_rest(r + 1, both)
+                    bias_rest(r + 1, (0,))
+                    bias_rest(r + 1, (1,))
+                bias_out(b)
                 mix_first(a)
                 if r == 0:
                     quantise(0, (1,))
                 mix_second(a)
-                if live(a + 2):
-                    transpose(a + 2)
-                    transpose(b + 2)
-                    regroup(a + 2)
-                    regroup(b + 2)
-                if live(a + 4):
-                    mask_rows(a + 4)
-                    mask_rows(b + 4)
+                if r >= 1 and live(a + 2):
+                    quantise(r + 1, both)
+                ahead = a + 2 if r == 0 else a + 4
+                if live(ahead):
+                    transpose(ahead)
+                    transpose(ahead + 1)
+                    regroup(ahead)
+                    regroup(ahead + 1)
+                if (a + 4) % GROUP == 0 and live(a + 4):
+                    mask_rows((a + 4) // GROUP)
+                project(b, (0,))
                 if live(a + 2):
                     bias_product(a + 2)
                     bias_out(a + 2)
-                project(b)
+                project(b, (1,))
                 mix_first(b)
-                if live(a + 2):
-                    quantise(r + 1, both)
+                if r == 0:
+                    quantise(1, both)
                 mix_second(b)
+                if r == 0:
+                    transpose(4)
+                    transpose(5)
+                    regroup(4)
+                    regroup(5)
                 if live(b + 2):
                     bias_product(b + 2)
-                    bias_out(b + 2)

@@ -24,9 +24,10 @@ WORDS = K // 2
 X_LOADS = (1, 1, 2) + (4,) * 7
 PAIR = 2
 N_ROUNDS = N_TILES // PAIR
+WARM_UPS = 4
 GROUP = 4
 ROWS = P // CLUSTERS
-E_PLAIN = 768
+E_PLAIN = 800
 E_REST = E - E_PLAIN
 
 FLOPS = 2 * BATCH * SEQ * CLUSTERS * K * E
@@ -96,6 +97,9 @@ def tile_model_pa_t_e_kernel(tc, attn_ctx, Wo_words, Wo_scales, bo, cluster_prob
 
         identity = const.tile([P, P], F32)
         make_identity(nc, identity[:])
+        proj = psum_acc.tile([P, BANK], F32)
+        for warm_up in range(WARM_UPS):
+            nc.tensor.matmul(out=proj[:, 0:P], lhsT=identity[:], rhs=identity[:], start=True, stop=True)
         probs = const.tile([P, CLUSTERS, ROWS], F32)
         nc.vector.memset(probs[:], 0.0)
         nc.vector.tensor_copy(out=probs[:, :, 0:N_TILES], in_=probs_bf[:].rearrange("p j c -> p c j"))
@@ -260,8 +264,7 @@ def tile_model_pa_t_e_kernel(tc, attn_ctx, Wo_words, Wo_scales, bo, cluster_prob
                 if r == 0:
                     bias_product(b)
                 if live(a + 2):
-                    bias_rest(r + 1, (0,))
-                    bias_rest(r + 1, (1,))
+                    bias_rest(r + 1, both)
                 bias_out(b)
                 mix_first(a)
                 if r == 0:

@@ -217,7 +217,7 @@ def tile_model_pa_t_e_kernel(tc, attn_ctx, Wo_words, Wo_scales, bo, cluster_prob
         def mix_first(j):
             partial = result.tile([P, E], F32)
             partial_of[j] = partial
-            for n in range(E_BANKS):
+            for n in reversed(range(E_BANKS)):
                 cols = slice(n * BANK, (n + 1) * BANK)
                 nc.vector.scalar_tensor_tensor(
                     out=partial[:, cols], in0=proj_of[(j, 0, n)][:], scalar=probs[:, 0, j : j + 1],
@@ -229,7 +229,7 @@ def tile_model_pa_t_e_kernel(tc, attn_ctx, Wo_words, Wo_scales, bo, cluster_prob
                 fused = result.tile([P, PAIR, E], F32)
                 fused_of[j // PAIR] = fused
             fused = fused_of[j // PAIR]
-            for n in range(E_BANKS):
+            for n in reversed(range(E_BANKS)):
                 cols = slice(n * BANK, (n + 1) * BANK)
                 nc.vector.scalar_tensor_tensor(
                     out=fused[:, j % PAIR, cols], in0=proj_of[(j, 1, n)][:], scalar=probs[:, 1, j : j + 1],
@@ -280,11 +280,10 @@ def tile_model_pa_t_e_kernel(tc, attn_ctx, Wo_words, Wo_scales, bo, cluster_prob
                     regroup(ahead + 1)
                 if (a + 4) % GROUP == 0 and live(a + 4):
                     mask_rows((a + 4) // GROUP)
-                project(b, (0,))
                 if live(a + 2):
                     bias_product(a + 2)
                     bias_out(a + 2)
-                project(b, (1,))
+                project(b, both)
                 mix_first(b)
                 if r == 0:
                     quantise(1, both)

@@ -217,7 +217,7 @@ def tile_model_pa_t_e_kernel(tc, attn_ctx, Wo_words, Wo_scales, bo, cluster_prob
         def mix_first(j):
             partial = result.tile([P, E], F32)
             partial_of[j] = partial
-            for n in reversed(range(E_BANKS)):
+            for n in range(E_BANKS):
                 cols = slice(n * BANK, (n + 1) * BANK)
                 nc.vector.scalar_tensor_tensor(
                     out=partial[:, cols], in0=proj_of[(j, 0, n)][:], scalar=probs[:, 0, j : j + 1],
@@ -229,7 +229,7 @@ def tile_model_pa_t_e_kernel(tc, attn_ctx, Wo_words, Wo_scales, bo, cluster_prob
                 fused = result.tile([P, PAIR, E], F32)
                 fused_of[j // PAIR] = fused
             fused = fused_of[j // PAIR]
-            for n in reversed(range(E_BANKS)):
+            for n in range(E_BANKS):
                 cols = slice(n * BANK, (n + 1) * BANK)
                 nc.vector.scalar_tensor_tensor(
                     out=fused[:, j % PAIR, cols], in0=proj_of[(j, 1, n)][:], scalar=probs[:, 1, j : j + 1],
@@ -257,41 +257,61 @@ def tile_model_pa_t_e_kernel(tc, attn_ctx, Wo_words, Wo_scales, bo, cluster_prob
             transpose(1)
             regroup(1)
             bias_rest(0, (1,))
-            for r in range(N_ROUNDS):
+            project(0, both)
+            bias_product(1)
+            bias_rest(1, both)
+            bias_out(1)
+            mix_first(0)
+            quantise(0, (1,))
+            mix_second(0)
+            transpose(2)
+            transpose(3)
+            regroup(2)
+            regroup(3)
+            mask_rows(1)
+            bias_product(2)
+            bias_out(2)
+            project(1, both)
+            mix_first(1)
+            quantise(1, both)
+            mix_second(1)
+            transpose(4)
+            transpose(5)
+            regroup(4)
+            regroup(5)
+            bias_product(3)
+            project(2, both)
+            bias_rest(2, both)
+            bias_out(3)
+            bias_product(4)
+            bias_out(4)
+            for r in range(1, N_ROUNDS):
                 a = PAIR * r
                 b = a + 1
-                project(a, both)
-                if r == 0:
-                    bias_product(b)
-                if live(a + 2):
-                    bias_rest(r + 1, both)
-                bias_out(b)
+                if live(a + 4):
+                    transpose(a + 4)
+                    transpose(a + 5)
                 mix_first(a)
-                if r == 0:
-                    quantise(0, (1,))
                 mix_second(a)
-                if r >= 1 and live(a + 2):
+                if live(a + 2):
                     quantise(r + 1, both)
-                ahead = a + 2 if r == 0 else a + 4
-                if live(ahead):
-                    transpose(ahead)
-                    transpose(ahead + 1)
-                    regroup(ahead)
-                    regroup(ahead + 1)
+                if live(a + 4):
+                    regroup(a + 4)
+                    regroup(a + 5)
                 if (a + 4) % GROUP == 0 and live(a + 4):
                     mask_rows((a + 4) // GROUP)
-                if live(a + 2):
-                    bias_product(a + 2)
-                    bias_out(a + 2)
-                project(b, both)
+                project(b, (0,))
+                if live(a + 3):
+                    bias_product(a + 3)
+                    bias_out(a + 3)
+                project(b, (1,))
                 mix_first(b)
-                if r == 0:
-                    quantise(1, both)
                 mix_second(b)
-                if r == 0:
-                    transpose(4)
-                    transpose(5)
-                    regroup(4)
-                    regroup(5)
-                if live(b + 2):
-                    bias_product(b + 2)
+                if live(a + 2):
+                    project(a + 2, (0,))
+                if live(a + 4):
+                    bias_rest(r + 2, both)
+                    bias_product(a + 4)
+                    bias_out(a + 4)
+                if live(a + 2):
+                    project(a + 2, (1,))

@@ -45,7 +45,7 @@ def tile_model_pa_t_e_kernel(tc, attn_ctx, Wo_words, Wo_scales, bo, cluster_prob
         x_pool = stack.enter_context(tc.tile_pool(name="x", bufs=1))
         quant = stack.enter_context(tc.tile_pool(name="quant", bufs=3))
         bias_pool = stack.enter_context(tc.tile_pool(name="bias", bufs=4))
-        result = stack.enter_context(tc.tile_pool(name="result", bufs=3))
+        result = stack.enter_context(tc.tile_pool(name="result", bufs=4))
         psum_x = stack.enter_context(tc.psum_pool(name="psum_x", bufs=2))
         psum_bias = stack.enter_context(tc.psum_pool(name="psum_bias", bufs=2))
         psum_acc = stack.enter_context(tc.psum_pool(name="psum_acc", bufs=4))
@@ -129,6 +129,7 @@ def tile_model_pa_t_e_kernel(tc, attn_ctx, Wo_words, Wo_scales, bo, cluster_prob
         bias_of = {}
         terms_of = {}
         fused_of = {}
+        scaled_of = {}
 
         def transpose(j):
             x_chunk, place = x_of[j]
@@ -167,22 +168,33 @@ def tile_model_pa_t_e_kernel(tc, attn_ctx, Wo_words, Wo_scales, bo, cluster_prob
 
         def bias_out(j):
             for first, width, bias_psum in bias_psum_of[j]:
-                nc.scalar.copy(out=bias_of[j // PAIR][:, j % PAIR, first : first + width], in_=bias_psum[:, 0:width])
+                nc.scalar.copy(out=bias_tile(j // PAIR)[:, j % PAIR, first : first + width], in_=bias_psum[:, 0:width])
 
-        def bias_rest(r, tiles):
+        def bias_tile(r):
             if r not in bias_of:
                 bias = bias_pool.tile([P, PAIR, E], F32)
+                bias_of[r] = bias
+            return bias_of[r]
+
+        def rest_terms(r, tiles):
+            if r not in terms_of:
                 bias0 = bias_pool.tile([P, PAIR, E_REST], F32)
                 bias1 = bias_pool.tile([P, PAIR, E_REST], F32)
-                bias_of[r] = bias
                 terms_of[r] = (bias0, bias1)
             bias0, bias1 = terms_of[r]
             for t in tiles:
                 j = PAIR * r + t
-                nc.scalar.activation(out=bias0[:, t, :], in_=bo_rest[:, 0, :], func=COPY, scale=probs[:, 0, j : j + 1])
-                nc.scalar.activation(out=bias1[:, t, :], in_=bo_rest[:, 1, :], func=COPY, scale=probs[:, 1, j : j + 1])
+                nc.gpsimd.tensor_scalar(out=bias0[:, t, :], in0=bo_rest[:, 0, :], scalar1=probs[:, 0, j : j + 1], scalar2=0.0, op0=MULT, op1=ADD)
+                nc.gpsimd.tensor_scalar(out=bias1[:, t, :], in0=bo_rest[:, 1, :], scalar1=probs[:, 1, j : j + 1], scalar2=0.0, op0=MULT, op1=ADD)
+
+        def rest_sum(r, tiles):
+            bias0, bias1 = terms_of[r]
             span = slice(tiles[0], tiles[-1] + 1)
-            nc.gpsimd.tensor_tensor(out=bias_of[r][:, span, E_PLAIN:E], in0=bias0[:, span, :], in1=bias1[:, span, :], op=ADD)
+            nc.gpsimd.tensor_tensor(out=bias_tile(r)[:, span, E_PLAIN:E], in0=bias0[:, span, :], in1=bias1[:, span, :], op=ADD)
+
+        def bias_rest(r, tiles):
+            rest_terms(r, tiles)
+            rest_sum(r, tiles)
 
         def quantise(r, tiles):
             if r not in codes_of:
@@ -224,6 +236,11 @@ def tile_model_pa_t_e_kernel(tc, attn_ctx, Wo_words, Wo_scales, bo, cluster_prob
                     in1=bias_of[j // PAIR][:, j % PAIR, cols], op0=MULT, op1=ADD,
                 )
 
+        def scale_bank(j, n):
+            scaled = result.tile([P, BANK], F32)
+            nc.scalar.activation(out=scaled[:], in_=proj_of[(j, 1, n)][:], func=COPY, scale=probs[:, 1, j : j + 1])
+            scaled_of[(j, n)] = scaled
+
         def mix_second(j):
             if j % PAIR == 0:
                 fused = result.tile([P, PAIR, E], F32)
@@ -231,6 +248,9 @@ def tile_model_pa_t_e_kernel(tc, attn_ctx, Wo_words, Wo_scales, bo, cluster_prob
             fused = fused_of[j // PAIR]
             for n in range(E_BANKS):
                 cols = slice(n * BANK, (n + 1) * BANK)
+                if (j, n) in scaled_of:
+                    nc.gpsimd.tensor_tensor(out=fused[:, j % PAIR, cols], in0=partial_of[j][:, cols], in1=scaled_of[(j, n)][:], op=ADD)
+                    continue
                 nc.vector.scalar_tensor_tensor(
                     out=fused[:, j % PAIR, cols], in0=proj_of[(j, 1, n)][:], scalar=probs[:, 1, j : j + 1],
                     in1=partial_of[j][:, cols], op0=MULT, op1=ADD,
@@ -282,6 +302,7 @@ def tile_model_pa_t_e_kernel(tc, attn_ctx, Wo_words, Wo_scales, bo, cluster_prob
             bias_product(3)
             project(2, both)
             bias_rest(2, both)
+            rest_terms(3, both)
             bias_out(3)
             bias_product(4)
             bias_out(4)
@@ -305,12 +326,17 @@ def tile_model_pa_t_e_kernel(tc, attn_ctx, Wo_words, Wo_scales, bo, cluster_prob
                     bias_product(a + 3)
                     bias_out(a + 3)
                 project(b, (1,))
+                if r < N_ROUNDS - 1:
+                    scale_bank(b, 1)
                 mix_first(b)
                 mix_second(b)
+                if live(a + 4):
+                    rest_sum(r + 2, both)
+                if live(a + 6):
+                    rest_terms(r + 3, both)
                 if live(a + 2):
                     project(a + 2, (0,))
                 if live(a + 4):
-                    bias_rest(r + 2, both)
                     bias_product(a + 4)
                     bias_out(a + 4)
                 if live(a + 2):

@@ -184,7 +184,7 @@ def tile_model_pa_t_e_kernel(tc, attn_ctx, Wo_words, Wo_scales, bo, cluster_prob
             bias0, bias1 = terms_of[r]
             for t in tiles:
                 j = PAIR * r + t
-                nc.gpsimd.tensor_scalar(out=bias0[:, t, :], in0=bo_rest[:, 0, :], scalar1=probs[:, 0, j : j + 1], scalar2=0.0, op0=MULT, op1=ADD)
+                nc.scalar.activation(out=bias0[:, t, :], in_=bo_rest[:, 0, :], func=COPY, scale=probs[:, 0, j : j + 1])
                 nc.gpsimd.tensor_scalar(out=bias1[:, t, :], in0=bo_rest[:, 1, :], scalar1=probs[:, 1, j : j + 1], scalar2=0.0, op0=MULT, op1=ADD)
 
         def rest_sum(r, tiles):

@@ -22,11 +22,12 @@ BANK = 512
 E_BANKS = E // BANK
 WORDS = K // 2
 X_LOADS = (1, 1, 2) + (4,) * 7
+EARLY_LOADS = 5
+LOAD_LEAD = 3
 PAIR = 2
 N_ROUNDS = N_TILES // PAIR
-WARM_UPS = 4
 GROUP = 4
-ROWS = P // CLUSTERS
+N_GROUPS = N_TILES // GROUP
 E_PLAIN = 800
 E_REST = E - E_PLAIN
 
@@ -51,15 +52,16 @@ def tile_model_pa_t_e_kernel(tc, attn_ctx, Wo_words, Wo_scales, bo, cluster_prob
         psum_acc = stack.enter_context(tc.psum_pool(name="psum_acc", bufs=4))
 
         x_of = {}
+        first_of_load = [sum(X_LOADS[:number]) for number in range(len(X_LOADS))]
 
-        def load_x(first, count):
+        def load_x(number):
+            first, count = first_of_load[number], X_LOADS[number]
             x_chunk = x_pool.tile([P, HALVES, count, K], BF16, name="x%d" % first)
             nc.sync.dma_start(out=x_chunk[:], in_=x_rows[:, :, first : first + count, :])
             for place in range(count):
                 x_of[first + place] = (x_chunk, place)
 
         w_scales = const.tile([P, CLUSTERS, E], U8, align_bytes=64)
-        nc.vector.memset(w_scales[:].bitcast(I32), 0)
         w_words = const.tile([P, CLUSTERS, E], U32, align_bytes=64)
 
         def load_w(c):
@@ -68,59 +70,28 @@ def tile_model_pa_t_e_kernel(tc, attn_ctx, Wo_words, Wo_scales, bo, cluster_prob
                 in_=Wo_words[c].rearrange("p n t -> p (n t)").bitcast(I32),
             )
 
-        first = 0
-        for number, count in enumerate(X_LOADS):
-            load_x(first, count)
-            first += count
-            if number == 0:
-                for quadrant in range(4):
-                    nc.sync.dma_start(
-                        out=w_scales[32 * quadrant : 32 * quadrant + 4].bitcast(I32),
-                        in_=Wo_scales[:, 4 * quadrant : 4 * quadrant + 4, :].rearrange("g r n -> r g n").bitcast(I32),
-                    )
-            if number < CLUSTERS:
-                load_w(number)
+        def load_w_scales():
+            for quadrant in range(4):
+                nc.sync.dma_start(
+                    out=w_scales[32 * quadrant : 32 * quadrant + 4].bitcast(I32),
+                    in_=Wo_scales[:, 4 * quadrant : 4 * quadrant + 4, :].rearrange("g r n -> r g n").bitcast(I32),
+                )
 
-        probs_bf = const.tile([P, N_TILES, CLUSTERS], BF16)
-        nc.scalar.dma_start(out=probs_bf[:].rearrange("p j c -> p (j c)"), in_=probs_rows)
-        bo_plain = const.tile([P, E_PLAIN], BF16)
+        probs_bf = const.tile([P, N_TILES * CLUSTERS], BF16)
+        WIDE = CLUSTERS * GROUP * (N_GROUPS - 1) + P
+        probs_wide = const.tile([P, WIDE], F32)
+        bo_rows = const.tile([P, GROUP, E_PLAIN], BF16)
+        rest_rows = const.tile([P, CLUSTERS, E_REST], BF16)
+        ones = const.tile([P, P], BF16)
         bo_rest = const.tile([P, CLUSTERS, E_REST], BF16)
-        for c in range(CLUSTERS):
-            nc.scalar.dma_start(
-                out=bo_plain[c * ROWS : (c + 1) * ROWS, :], in_=bo[c, 0:E_PLAIN].partition_broadcast(ROWS)
-            )
-            nc.scalar.dma_start(out=bo_rest[:, c, :], in_=bo[c, E_PLAIN:E].partition_broadcast(P))
-
+        probs_t = const.tile([P, N_GROUPS, P], BF16)
         warm = const.tile([P, 2], F32)
-        nc.vector.memset(warm[:], 0.0)
-        nc.scalar.activation(out=warm[:, 1:2], in_=warm[:, 0:1], func=COPY)
-
         identity = const.tile([P, P], F32)
-        make_identity(nc, identity[:])
-        proj = psum_acc.tile([P, BANK], F32)
-        for warm_up in range(WARM_UPS):
-            nc.tensor.matmul(out=proj[:, 0:P], lhsT=identity[:], rhs=identity[:], start=True, stop=True)
-        probs = const.tile([P, CLUSTERS, ROWS], F32)
-        nc.vector.memset(probs[:], 0.0)
-        nc.vector.tensor_copy(out=probs[:, :, 0:N_TILES], in_=probs_bf[:].rearrange("p j c -> p c j"))
-        probs_t_psum = psum_bias.tile([P, BANK], F32, tag="bias_psum")
-        nc.tensor.transpose(probs_t_psum[:, 0:P], probs[:].rearrange("p c j -> p (c j)"), identity[:])
-        probs_t = const.tile([P, P], BF16)
-        nc.vector.tensor_copy(out=probs_t[:], in_=probs_t_psum[:, 0:P])
-        row_of_tile = const.tile([P, N_TILES], F32)
-        nc.vector.tensor_tensor(
-            out=row_of_tile[:], in0=identity[:, 0:N_TILES], in1=identity[:, ROWS : ROWS + N_TILES], op=ADD
-        )
-        rows_of_group = const.tile([P, N_TILES // GROUP], F32)
-        nc.vector.tensor_reduce(out=rows_of_group[:], in_=row_of_tile[:].rearrange("p (g t) -> p g t", t=GROUP), axis=AXIS_X, op=ADD)
-        rows_of_place = const.tile([P, GROUP], F32)
-        nc.vector.tensor_reduce(out=rows_of_place[:], in_=row_of_tile[:].rearrange("p (g t) -> p t g", t=GROUP), axis=AXIS_X, op=ADD)
-        bo_place = const.tile([P, GROUP, E_PLAIN], BF16)
-        for t in range(GROUP):
-            nc.vector.tensor_scalar_mul(out=bo_place[:, t, :], in0=bo_plain[:], scalar1=rows_of_place[:, t : t + 1])
+
+        def weight(c, j):
+            return probs_wide[:, CLUSTERS * j + c : CLUSTERS * j + c + 1]
 
         xt_of = {}
-        masked_of = {}
         bias_psum_of = {}
         proj_of = {}
         partial_of = {}
@@ -129,6 +100,7 @@ def tile_model_pa_t_e_kernel(tc, attn_ctx, Wo_words, Wo_scales, bo, cluster_prob
         bias_of = {}
         terms_of = {}
         fused_of = {}
+        window_of = {}
         scaled_of = {}
 
         def transpose(j):
@@ -150,10 +122,16 @@ def tile_model_pa_t_e_kernel(tc, attn_ctx, Wo_words, Wo_scales, bo, cluster_prob
                 in_=xt_of[j][:].rearrange("p s (b c) -> p c b s", c=CLUSTERS),
             )
 
-        def mask_rows(g):
-            probs_t_g = bias_pool.tile([P, P], BF16)
-            nc.scalar.activation(out=probs_t_g[:], in_=probs_t[:], func=COPY, scale=rows_of_group[:, g : g + 1])
-            masked_of[g] = probs_t_g
+        def windows(groups):
+            window = psum_acc.tile([P, BANK], F32, tag="proj")
+            for place, g in enumerate(groups):
+                first = CLUSTERS * GROUP * g
+                nc.tensor.transpose(window[:, place * P : (place + 1) * P], probs_wide[:, first : first + P], identity[:])
+            window_of[groups[0]] = window
+
+        def windows_out(groups, engine):
+            width = len(groups) * P
+            engine(out=probs_t[:, groups[0] : groups[-1] + 1, :].rearrange("p g m -> p (g m)"), in_=window_of[groups[0]][:, 0:width])
 
         def bias_product(j):
             banks = []
@@ -161,14 +139,10 @@ def tile_model_pa_t_e_kernel(tc, attn_ctx, Wo_words, Wo_scales, bo, cluster_prob
                 width = min(BANK, E_PLAIN - first)
                 bias_psum = psum_bias.tile([P, BANK], F32)
                 nc.tensor.matmul(
-                    out=bias_psum[:, 0:width], lhsT=masked_of[j // GROUP][:], rhs=bo_place[:, j % GROUP, first : first + width], start=True, stop=True
+                    out=bias_psum[:, 0:width], lhsT=probs_t[:, j // GROUP, :], rhs=bo_rows[:, j % GROUP, first : first + width], start=True, stop=True
                 )
                 banks.append((first, width, bias_psum))
             bias_psum_of[j] = banks
-
-        def bias_out(j):
-            for first, width, bias_psum in bias_psum_of[j]:
-                nc.scalar.copy(out=bias_tile(j // PAIR)[:, j % PAIR, first : first + width], in_=bias_psum[:, 0:width])
 
         def bias_tile(r):
             if r not in bias_of:
@@ -176,24 +150,31 @@ def tile_model_pa_t_e_kernel(tc, attn_ctx, Wo_words, Wo_scales, bo, cluster_prob
                 bias_of[r] = bias
             return bias_of[r]
 
-        def rest_terms(r, tiles):
+        def bias_out(j):
+            for first, width, bias_psum in bias_psum_of[j]:
+                nc.scalar.copy(out=bias_tile(j // PAIR)[:, j % PAIR, first : first + width], in_=bias_psum[:, 0:width])
+
+        def rest_terms(r, tiles, on_gpsimd=(False, True), source=None):
             if r not in terms_of:
                 bias0 = bias_pool.tile([P, PAIR, E_REST], F32)
                 bias1 = bias_pool.tile([P, PAIR, E_REST], F32)
                 terms_of[r] = (bias0, bias1)
-            bias0, bias1 = terms_of[r]
             for t in tiles:
                 j = PAIR * r + t
-                nc.scalar.activation(out=bias0[:, t, :], in_=bo_rest[:, 0, :], func=COPY, scale=probs[:, 0, j : j + 1])
-                nc.gpsimd.tensor_scalar(out=bias1[:, t, :], in0=bo_rest[:, 1, :], scalar1=probs[:, 1, j : j + 1], scalar2=0.0, op0=MULT, op1=ADD)
+                for c in range(CLUSTERS):
+                    rows = bo_rest[:, c, :] if source is None else source[:, c * E_REST : (c + 1) * E_REST]
+                    if on_gpsimd[c]:
+                        nc.gpsimd.tensor_scalar(out=terms_of[r][c][:, t, :], in0=rows, scalar1=weight(c, j), scalar2=0.0, op0=MULT, op1=ADD)
+                    else:
+                        nc.scalar.activation(out=terms_of[r][c][:, t, :], in_=rows, func=COPY, scale=weight(c, j))
 
         def rest_sum(r, tiles):
             bias0, bias1 = terms_of[r]
             span = slice(tiles[0], tiles[-1] + 1)
             nc.gpsimd.tensor_tensor(out=bias_tile(r)[:, span, E_PLAIN:E], in0=bias0[:, span, :], in1=bias1[:, span, :], op=ADD)
 
-        def bias_rest(r, tiles):
-            rest_terms(r, tiles)
+        def bias_rest(r, tiles, on_gpsimd=(True, True), source=None):
+            rest_terms(r, tiles, on_gpsimd, source)
             rest_sum(r, tiles)
 
         def quantise(r, tiles):
@@ -232,13 +213,13 @@ def tile_model_pa_t_e_kernel(tc, attn_ctx, Wo_words, Wo_scales, bo, cluster_prob
             for n in range(E_BANKS):
                 cols = slice(n * BANK, (n + 1) * BANK)
                 nc.vector.scalar_tensor_tensor(
-                    out=partial[:, cols], in0=proj_of[(j, 0, n)][:], scalar=probs[:, 0, j : j + 1],
+                    out=partial[:, cols], in0=proj_of[(j, 0, n)][:], scalar=weight(0, j),
                     in1=bias_of[j // PAIR][:, j % PAIR, cols], op0=MULT, op1=ADD,
                 )
 
         def scale_bank(j, n):
             scaled = result.tile([P, BANK], F32)
-            nc.scalar.activation(out=scaled[:], in_=proj_of[(j, 1, n)][:], func=COPY, scale=probs[:, 1, j : j + 1])
+            nc.scalar.activation(out=scaled[:], in_=proj_of[(j, 1, n)][:], func=COPY, scale=weight(1, j))
             scaled_of[(j, n)] = scaled
 
         def mix_second(j):
@@ -252,7 +233,7 @@ def tile_model_pa_t_e_kernel(tc, attn_ctx, Wo_words, Wo_scales, bo, cluster_prob
                     nc.gpsimd.tensor_tensor(out=fused[:, j % PAIR, cols], in0=partial_of[j][:, cols], in1=scaled_of[(j, n)][:], op=ADD)
                     continue
                 nc.vector.scalar_tensor_tensor(
-                    out=fused[:, j % PAIR, cols], in0=proj_of[(j, 1, n)][:], scalar=probs[:, 1, j : j + 1],
+                    out=fused[:, j % PAIR, cols], in0=proj_of[(j, 1, n)][:], scalar=weight(1, j),
                     in1=partial_of[j][:, cols], op0=MULT, op1=ADD,
                 )
                 if j == N_TILES - 1:
@@ -267,48 +248,86 @@ def tile_model_pa_t_e_kernel(tc, attn_ctx, Wo_words, Wo_scales, bo, cluster_prob
 
         both = (0, 1)
         with tc.manual_schedule():
-            mask_rows(0)
+            load_x(0)
+            nc.scalar.dma_start(out=probs_bf[:], in_=probs_rows)
+            nc.vector.memset(w_scales[:].bitcast(I32), 0)
+            load_w_scales()
+            load_w(0)
+            load_x(1)
+            load_w(1)
+            for number in range(2, EARLY_LOADS):
+                load_x(number)
+            nc.vector.memset(bo_rows[:, 0, :].bitcast(I32), 0)
+            nc.scalar.dma_start(out=bo_rows[0:CLUSTERS, 0, :], in_=bo[:, 0:E_PLAIN])
+            nc.vector.memset(rest_rows[:].rearrange("p c e -> p (c e)").bitcast(I32), 0)
+            for c in range(CLUSTERS):
+                nc.scalar.dma_start(out=rest_rows[c : c + 1, c, :], in_=bo[c : c + 1, E_PLAIN:E])
+            nc.vector.memset(warm[:], 0.0)
+            nc.scalar.activation(out=warm[:, 1:2], in_=warm[:, 0:1], func=COPY)
+            make_identity(nc, identity[:])
+            nc.vector.memset(probs_wide[:], 0.0)
+            nc.vector.memset(ones[:], 1.0)
+            for t in range(1, GROUP):
+                nc.vector.memset(bo_rows[:, t, :].bitcast(I32), 0)
+                nc.scalar.dma_start(out=bo_rows[CLUSTERS * t : CLUSTERS * (t + 1), t, :], in_=bo[:, 0:E_PLAIN])
+            nc.vector.tensor_copy(out=probs_wide[:, 0 : N_TILES * CLUSTERS], in_=probs_bf[:])
+
+            windows((0,))
+            windows_out((0,), nc.vector.tensor_copy)
             transpose(0)
+            spread = psum_acc.tile([P, BANK], F32, tag="proj")
+            nc.tensor.matmul(out=spread[:, 0 : CLUSTERS * E_REST], lhsT=ones[:], rhs=rest_rows[:].rearrange("p c e -> p (c e)"), start=True, stop=True)
             regroup(0)
             quantise(0, (0,))
-            bias_rest(0, (0,))
             bias_product(0)
+            bias_rest(0, (0,), on_gpsimd=(False, False), source=spread)
             bias_out(0)
-            transpose(1)
-            regroup(1)
+            nc.vector.tensor_copy(out=bo_rest[:].rearrange("p c e -> p (c e)"), in_=spread[:, 0 : CLUSTERS * E_REST])
+            windows((1, 2, 3))
+            windows((4, 5, 6, 7))
+            windows_out((1, 2, 3), nc.vector.tensor_copy)
+            windows_out((4, 5, 6, 7), nc.scalar.copy)
             bias_rest(0, (1,))
-            project(0, both)
-            bias_product(1)
             bias_rest(1, both)
-            bias_out(1)
+            project(0, (0,))
+            transpose(1)
+            bias_product(1)
+            regroup(1)
             mix_first(0)
             quantise(0, (1,))
+            project(0, (1,))
+            bias_out(1)
             mix_second(0)
+            project(1, (0,))
             transpose(2)
             transpose(3)
+            bias_product(2)
+            project(1, (1,))
             regroup(2)
             regroup(3)
-            mask_rows(1)
-            bias_product(2)
             bias_out(2)
-            project(1, both)
             mix_first(1)
-            quantise(1, both)
+            quantise(1, (0,))
             mix_second(1)
+            quantise(1, (1,))
+            bias_rest(2, both)
+            rest_terms(3, both, on_gpsimd=(True, True))
+            project(2, (0,))
             transpose(4)
             transpose(5)
+            bias_product(3)
+            project(2, (1,))
             regroup(4)
             regroup(5)
-            bias_product(3)
-            project(2, both)
-            bias_rest(2, both)
-            rest_terms(3, both)
             bias_out(3)
             bias_product(4)
             bias_out(4)
             for r in range(1, N_ROUNDS):
                 a = PAIR * r
                 b = a + 1
+                for number in range(EARLY_LOADS, len(X_LOADS)):
+                    if first_of_load[number] == a + 4 + PAIR * LOAD_LEAD:
+                        load_x(number)
                 if live(a + 4):
                     transpose(a + 4)
                     transpose(a + 5)
@@ -319,8 +338,6 @@ def tile_model_pa_t_e_kernel(tc, attn_ctx, Wo_words, Wo_scales, bo, cluster_prob
                 if live(a + 4):
                     regroup(a + 4)
                     regroup(a + 5)
-                if (a + 4) % GROUP == 0 and live(a + 4):
-                    mask_rows((a + 4) // GROUP)
                 project(b, (0,))
                 if live(a + 3):
                     bias_product(a + 3)

@@ -26,6 +26,8 @@ EARLY_LOADS = 5
 LOAD_LEAD = 3
 PAIR = 2
 N_ROUNDS = N_TILES // PAIR
+LAST_PIECE = 128
+FINE_TILES = 4
 GROUP = 4
 N_GROUPS = N_TILES // GROUP
 E_PLAIN = 800
@@ -112,14 +114,15 @@ def tile_model_pa_t_e_kernel(tc, attn_ctx, Wo_words, Wo_scales, bo, cluster_prob
                     nc.tensor.transpose(xt[:, 2 * half + u, :], x_words[:, half, place, u:WORDS:2], identity[:])
             xt_of[j] = xt
 
-        def regroup(j):
-            if j % PAIR == 0:
+        def regroup(j, clusters=(0, 1)):
+            if j // PAIR not in grouped_of:
                 grouped = quant.tile([P, PAIR, CLUSTERS * P * 4], BF16, align_bytes=64)
                 grouped_of[j // PAIR] = grouped
             grouped = grouped_of[j // PAIR]
+            span = slice(clusters[0], clusters[-1] + 1)
             nc.scalar.copy(
-                out=grouped[:, j % PAIR, :].bitcast(F32).rearrange("p (c b s) -> p c b s", c=CLUSTERS, s=2 * HALVES),
-                in_=xt_of[j][:].rearrange("p s (b c) -> p c b s", c=CLUSTERS),
+                out=grouped[:, j % PAIR, :].bitcast(F32).rearrange("p (c b s) -> p c b s", c=CLUSTERS, s=2 * HALVES)[:, span],
+                in_=xt_of[j][:].rearrange("p s (b c) -> p c b s", c=CLUSTERS)[:, span],
             )
 
         def windows(groups):
@@ -177,6 +180,20 @@ def tile_model_pa_t_e_kernel(tc, attn_ctx, Wo_words, Wo_scales, bo, cluster_prob
             rest_terms(r, tiles, on_gpsimd, source)
             rest_sum(r, tiles)
 
+        def quantise_cluster(j, c):
+            r = j // PAIR
+            if r not in codes_of:
+                codes = quant.tile([P, PAIR * CLUSTERS, P], U32, align_bytes=64)
+                scales = quant.tile([P, PAIR * CLUSTERS, P], U8, align_bytes=64)
+                codes_of[r] = (codes, scales)
+            codes, scales = codes_of[r]
+            slot = (j % PAIR) * CLUSTERS + c
+            nc.vector.quantize_mx(
+                out=codes[:, slot, :].bitcast(FP8X4),
+                scales=scales[:, slot, :],
+                in_=grouped_of[r][:, j % PAIR, c * P * 4 : (c + 1) * P * 4],
+            )
+
         def quantise(r, tiles):
             if r not in codes_of:
                 codes = quant.tile([P, PAIR * CLUSTERS, P], U32, align_bytes=64)
@@ -227,20 +244,23 @@ def tile_model_pa_t_e_kernel(tc, attn_ctx, Wo_words, Wo_scales, bo, cluster_prob
                 fused = result.tile([P, PAIR, E], F32)
                 fused_of[j // PAIR] = fused
             fused = fused_of[j // PAIR]
+            fine = j >= N_TILES - FINE_TILES
             for n in range(E_BANKS):
-                cols = slice(n * BANK, (n + 1) * BANK)
-                if (j, n) in scaled_of:
-                    nc.gpsimd.tensor_tensor(out=fused[:, j % PAIR, cols], in0=partial_of[j][:, cols], in1=scaled_of[(j, n)][:], op=ADD)
-                    continue
-                nc.vector.scalar_tensor_tensor(
-                    out=fused[:, j % PAIR, cols], in0=proj_of[(j, 1, n)][:], scalar=weight(1, j),
-                    in1=partial_of[j][:, cols], op0=MULT, op1=ADD,
-                )
-                if j == N_TILES - 1:
-                    nc.sync.dma_start(out=out_rows[:, j, cols], in_=fused[:, j % PAIR, cols])
-            if j == N_TILES - PAIR:
-                nc.sync.dma_start(out=out_rows[:, j, :], in_=fused[:, j % PAIR, :])
-            elif j % PAIR == PAIR - 1 and j < N_TILES - 1:
+                pieces = (BANK - LAST_PIECE, LAST_PIECE) if (j, n) == (N_TILES - 1, E_BANKS - 1) else (BANK,)
+                first = n * BANK
+                for width in pieces:
+                    cols = slice(first, first + width)
+                    if (j, n) in scaled_of:
+                        nc.gpsimd.tensor_tensor(out=fused[:, j % PAIR, cols], in0=partial_of[j][:, cols], in1=scaled_of[(j, n)][:], op=ADD)
+                    else:
+                        nc.vector.scalar_tensor_tensor(
+                            out=fused[:, j % PAIR, cols], in0=proj_of[(j, 1, n)][:, first - n * BANK : first - n * BANK + width], scalar=weight(1, j),
+                            in1=partial_of[j][:, cols], op0=MULT, op1=ADD,
+                        )
+                    if fine:
+                        nc.sync.dma_start(out=out_rows[:, j, cols], in_=fused[:, j % PAIR, cols])
+                    first += width
+            if j % PAIR == PAIR - 1 and not fine:
                 nc.sync.dma_start(out=out_rows[:, j - PAIR + 1 : j + 1, :], in_=fused[:])
 
         def live(j):
@@ -275,10 +295,12 @@ def tile_model_pa_t_e_kernel(tc, attn_ctx, Wo_words, Wo_scales, bo, cluster_prob
             windows((0,))
             windows_out((0,), nc.vector.tensor_copy)
             transpose(0)
+            regroup(0, (0,))
+            quantise_cluster(0, 0)
+            regroup(0, (1,))
+            quantise_cluster(0, 1)
             spread = psum_acc.tile([P, BANK], F32, tag="proj")
             nc.tensor.matmul(out=spread[:, 0 : CLUSTERS * E_REST], lhsT=ones[:], rhs=rest_rows[:].rearrange("p c e -> p (c e)"), start=True, stop=True)
-            regroup(0)
-            quantise(0, (0,))
             bias_product(0)
             bias_rest(0, (0,), on_gpsimd=(False, False), source=spread)
             bias_out(0)
@@ -331,6 +353,8 @@ def tile_model_pa_t_e_kernel(tc, attn_ctx, Wo_words, Wo_scales, bo, cluster_prob
                 if live(a + 4):
                     transpose(a + 4)
                     transpose(a + 5)
+                if r == N_ROUNDS - 1:
+                    scale_bank(a, 1)
                 mix_first(a)
                 mix_second(a)
                 if live(a + 2):

@@ -56,10 +56,10 @@ def tile_model_pa_t_e_kernel(tc, attn_ctx, Wo_words, Wo_scales, bo, cluster_prob
         x_of = {}
         first_of_load = [sum(X_LOADS[:number]) for number in range(len(X_LOADS))]
 
-        def load_x(number):
+        def load_x(number, queue=nc.sync):
             first, count = first_of_load[number], X_LOADS[number]
             x_chunk = x_pool.tile([P, HALVES, count, K], BF16, name="x%d" % first)
-            nc.sync.dma_start(out=x_chunk[:], in_=x_rows[:, :, first : first + count, :])
+            queue.dma_start(out=x_chunk[:], in_=x_rows[:, :, first : first + count, :])
             for place in range(count):
                 x_of[first + place] = (x_chunk, place)
 
@@ -82,9 +82,8 @@ def tile_model_pa_t_e_kernel(tc, attn_ctx, Wo_words, Wo_scales, bo, cluster_prob
         probs_bf = const.tile([P, N_TILES * CLUSTERS], BF16)
         WIDE = CLUSTERS * GROUP * (N_GROUPS - 1) + P
         probs_wide = const.tile([P, WIDE], F32)
-        bo_rows = const.tile([P, GROUP, E_PLAIN], BF16)
-        rest_rows = const.tile([P, CLUSTERS, E_REST], BF16)
-        ones = const.tile([P, P], BF16)
+        bo_rows = const.tile([P, GROUP, E], BF16)
+        row_picker = const.tile([P, CLUSTERS], BF16)
         bo_rest = const.tile([P, CLUSTERS, E_REST], BF16)
         probs_t = const.tile([P, N_GROUPS, P], BF16)
         warm = const.tile([P, 2], F32)
@@ -268,28 +267,25 @@ def tile_model_pa_t_e_kernel(tc, attn_ctx, Wo_words, Wo_scales, bo, cluster_prob
 
         both = (0, 1)
         with tc.manual_schedule():
-            load_x(0)
             nc.scalar.dma_start(out=probs_bf[:], in_=probs_rows)
+            load_x(0)
+            load_w(0)
+            nc.vector.memset(bo_rows[:, 0, :].bitcast(I32), 0)
+            nc.scalar.dma_start(out=bo_rows[0:CLUSTERS, 0, :], in_=bo[:, :])
             nc.vector.memset(w_scales[:].bitcast(I32), 0)
             load_w_scales()
-            load_w(0)
             load_x(1)
             load_w(1)
             for number in range(2, EARLY_LOADS):
                 load_x(number)
-            nc.vector.memset(bo_rows[:, 0, :].bitcast(I32), 0)
-            nc.scalar.dma_start(out=bo_rows[0:CLUSTERS, 0, :], in_=bo[:, 0:E_PLAIN])
-            nc.vector.memset(rest_rows[:].rearrange("p c e -> p (c e)").bitcast(I32), 0)
-            for c in range(CLUSTERS):
-                nc.scalar.dma_start(out=rest_rows[c : c + 1, c, :], in_=bo[c : c + 1, E_PLAIN:E])
             nc.vector.memset(warm[:], 0.0)
             nc.scalar.activation(out=warm[:, 1:2], in_=warm[:, 0:1], func=COPY)
             make_identity(nc, identity[:])
             nc.vector.memset(probs_wide[:], 0.0)
-            nc.vector.memset(ones[:], 1.0)
             for t in range(1, GROUP):
-                nc.vector.memset(bo_rows[:, t, :].bitcast(I32), 0)
-                nc.scalar.dma_start(out=bo_rows[CLUSTERS * t : CLUSTERS * (t + 1), t, :], in_=bo[:, 0:E_PLAIN])
+                nc.vector.memset(bo_rows[:, t, 0:E_PLAIN].bitcast(I32), 0)
+                nc.scalar.dma_start(out=bo_rows[CLUSTERS * t : CLUSTERS * (t + 1), t, 0:E_PLAIN], in_=bo[:, 0:E_PLAIN])
+            nc.vector.tensor_copy(out=row_picker[:], in_=identity[:, 0:CLUSTERS])
             nc.vector.tensor_copy(out=probs_wide[:, 0 : N_TILES * CLUSTERS], in_=probs_bf[:])
 
             windows((0,))
@@ -300,7 +296,10 @@ def tile_model_pa_t_e_kernel(tc, attn_ctx, Wo_words, Wo_scales, bo, cluster_prob
             regroup(0, (1,))
             quantise_cluster(0, 1)
             spread = psum_acc.tile([P, BANK], F32, tag="proj")
-            nc.tensor.matmul(out=spread[:, 0 : CLUSTERS * E_REST], lhsT=ones[:], rhs=rest_rows[:].rearrange("p c e -> p (c e)"), start=True, stop=True)
+            for c in range(CLUSTERS):
+                nc.tensor.matmul(
+                    out=spread[:, c * E_REST : (c + 1) * E_REST], lhsT=row_picker[:, c : c + 1].to_broadcast([P, P]), rhs=bo_rows[:, 0, E_PLAIN:E], start=True, stop=True
+                )
             bias_product(0)
             bias_rest(0, (0,), on_gpsimd=(False, False), source=spread)
             bias_out(0)

@@ -103,6 +103,7 @@ def tile_model_pa_t_e_kernel(tc, attn_ctx, Wo_words, Wo_scales, bo, cluster_prob
         fused_of = {}
         window_of = {}
         scaled_of = {}
+        first_done = set()
 
         def transpose(j):
             x_chunk, place = x_of[j]
@@ -206,11 +207,11 @@ def tile_model_pa_t_e_kernel(tc, attn_ctx, Wo_words, Wo_scales, bo, cluster_prob
                 in_=grouped_of[r][:, tiles[0] : tiles[-1] + 1, :].rearrange("p t k -> p (t k)"),
             )
 
-        def project(j, clusters):
+        def project(j, clusters, banks=(0, 1)):
             codes, scales = codes_of[j // PAIR]
             for c in clusters:
                 slot = (j % PAIR) * CLUSTERS + c
-                for n in range(E_BANKS):
+                for n in banks:
                     proj = psum_acc.tile([P, BANK], F32)
                     nc.tensor.matmul_mx(
                         out=proj[:],
@@ -223,13 +224,17 @@ def tile_model_pa_t_e_kernel(tc, attn_ctx, Wo_words, Wo_scales, bo, cluster_prob
                     )
                     proj_of[(j, c, n)] = proj
 
-        def mix_first(j):
-            partial = result.tile([P, E], F32)
-            partial_of[j] = partial
-            for n in range(E_BANKS):
+        def mix_first(j, banks=(0, 1)):
+            if j not in partial_of:
+                partial = result.tile([P, E], F32)
+                partial_of[j] = partial
+            for n in banks:
+                if (j, n) in first_done:
+                    continue
+                first_done.add((j, n))
                 cols = slice(n * BANK, (n + 1) * BANK)
                 nc.vector.scalar_tensor_tensor(
-                    out=partial[:, cols], in0=proj_of[(j, 0, n)][:], scalar=weight(0, j),
+                    out=partial_of[j][:, cols], in0=proj_of[(j, 0, n)][:], scalar=weight(0, j),
                     in1=bias_of[j // PAIR][:, j % PAIR, cols], op0=MULT, op1=ADD,
                 )
 
@@ -346,13 +351,14 @@ def tile_model_pa_t_e_kernel(tc, attn_ctx, Wo_words, Wo_scales, bo, cluster_prob
             for r in range(1, N_ROUNDS):
                 a = PAIR * r
                 b = a + 1
+                split = r < N_ROUNDS - 1
                 for number in range(EARLY_LOADS, len(X_LOADS)):
                     if first_of_load[number] == a + 4 + PAIR * LOAD_LEAD:
                         load_x(number)
                 if live(a + 4):
                     transpose(a + 4)
                     transpose(a + 5)
-                if r == N_ROUNDS - 1:
+                if not split:
                     scale_bank(a, 1)
                 mix_first(a)
                 mix_second(a)
@@ -360,22 +366,26 @@ def tile_model_pa_t_e_kernel(tc, attn_ctx, Wo_words, Wo_scales, bo, cluster_prob
                     quantise(r + 1, both)
                 if live(a + 4):
                     regroup(a + 4)
+                if split:
+                    project(b, (1,), (0,))
+                    scale_bank(b, 0)
+                if live(a + 4):
                     regroup(a + 5)
                 project(b, (0,))
                 if live(a + 3):
                     bias_product(a + 3)
                     bias_out(a + 3)
-                project(b, (1,))
-                if r < N_ROUNDS - 1:
-                    scale_bank(b, 1)
+                project(b, (1,), (1,) if split else (0, 1))
                 mix_first(b)
+                if live(a + 2):
+                    project(a + 2, (0,))
+                if split:
+                    mix_first(a + 2, (0,))
                 mix_second(b)
                 if live(a + 4):
                     rest_sum(r + 2, both)
                 if live(a + 6):
                     rest_terms(r + 3, both)
-                if live(a + 2):
-                    project(a + 2, (0,))
                 if live(a + 4):
                     bias_product(a + 4)
                     bias_out(a + 4)

@@ -385,7 +385,8 @@ def tile_model_pa_t_e_kernel(tc, attn_ctx, Wo_words, Wo_scales, bo, cluster_prob
                 if live(a + 4):
                     rest_sum(r + 2, both)
                 if live(a + 6):
-                    rest_terms(r + 3, both)
+                    rest_terms(r + 3, (0,), on_gpsimd=(False, False))
+                    rest_terms(r + 3, (1,))
                 if live(a + 4):
                     bias_product(a + 4)
                     bias_out(a + 4)

from contextlib import ExitStack

import concourse.mybir as mybir
from concourse.masks import make_identity

F32 = mybir.dt.float32
BF16 = mybir.dt.bfloat16
I32 = mybir.dt.int32
U32 = mybir.dt.uint32
U8 = mybir.dt.uint8
FP8X4 = mybir.dt.float8_e4m3fn_x4
MULT = mybir.AluOpType.mult
ADD = mybir.AluOpType.add
COPY = mybir.ActivationFunctionType.Copy
AXIS_X = mybir.AxisListType.X

P = 128
BATCH, SEQ, CLUSTERS, K, E = 64, 64, 2, 512, 1024
HALVES = 2
N_TILES = SEQ // HALVES
BANK = 512
E_BANKS = E // BANK
WORDS = K // 2
X_LOADS = (1, 1, 2) + (4,) * 7
EARLY_LOADS = 5
LOAD_LEAD = 3
PAIR = 2
N_ROUNDS = N_TILES // PAIR
LAST_PIECE = 128
FINE_TILES = 4
GROUP = 4
N_GROUPS = N_TILES // GROUP
E_PLAIN = 800
E_REST = E - E_PLAIN

FLOPS = 2 * BATCH * SEQ * CLUSTERS * K * E


def tile_model_pa_t_e_kernel(tc, attn_ctx, Wo_words, Wo_scales, bo, cluster_probs, out):
    nc = tc.nc

    x_rows = attn_ctx.rearrange("b c (half j) h d -> (b c) half j (h d)", half=HALVES)
    probs_rows = cluster_probs.rearrange("b (half j) c -> (b half) (j c)", half=HALVES)
    out_rows = out.rearrange("b (half j) e -> (b half) j e", half=HALVES)

    with ExitStack() as stack:
        const = stack.enter_context(tc.tile_pool(name="const", bufs=1))
        x_pool = stack.enter_context(tc.tile_pool(name="x", bufs=1))
        quant = stack.enter_context(tc.tile_pool(name="quant", bufs=3))
        bias_pool = stack.enter_context(tc.tile_pool(name="bias", bufs=4))
        result = stack.enter_context(tc.tile_pool(name="result", bufs=4))
        psum_x = stack.enter_context(tc.psum_pool(name="psum_x", bufs=2))
        psum_bias = stack.enter_context(tc.psum_pool(name="psum_bias", bufs=2))
        psum_acc = stack.enter_context(tc.psum_pool(name="psum_acc", bufs=4))

        x_of = {}
        first_of_load = [sum(X_LOADS[:number]) for number in range(len(X_LOADS))]

        def load_x(number, queue=nc.sync):
            first, count = first_of_load[number], X_LOADS[number]
            x_chunk = x_pool.tile([P, HALVES, count, K], BF16, name="x%d" % first)
            queue.dma_start(out=x_chunk[:], in_=x_rows[:, :, first : first + count, :])
            for place in range(count):
                x_of[first + place] = (x_chunk, place)

        w_scales = const.tile([P, CLUSTERS, E], U8, align_bytes=64)
        w_words = const.tile([P, CLUSTERS, E], U32, align_bytes=64)

        def load_w(c):
            nc.sync.dma_start(
                out=w_words[:, c, :].bitcast(I32),
                in_=Wo_words[c].rearrange("p n t -> p (n t)").bitcast(I32),
            )

        def load_w_scales():
            for quadrant in range(4):
                nc.sync.dma_start(
                    out=w_scales[32 * quadrant : 32 * quadrant + 4].bitcast(I32),
                    in_=Wo_scales[:, 4 * quadrant : 4 * quadrant + 4, :].rearrange("g r n -> r g n").bitcast(I32),
                )

        probs_bf = const.tile([P, N_TILES * CLUSTERS], BF16)
        WIDE = CLUSTERS * GROUP * (N_GROUPS - 1) + P
        probs_wide = const.tile([P, WIDE], F32)
        bo_rows = const.tile([P, GROUP, E], BF16)
        row_picker = const.tile([P, CLUSTERS], BF16)
        bo_rest = const.tile([P, CLUSTERS, E_REST], BF16)
        probs_t = const.tile([P, N_GROUPS, P], BF16)
        warm = const.tile([P, 2], F32)
        identity = const.tile([P, P], F32)

        def weight(c, j):
            return probs_wide[:, CLUSTERS * j + c : CLUSTERS * j + c + 1]

        xt_of = {}
        bias_psum_of = {}
        proj_of = {}
        partial_of = {}
        grouped_of = {}
        codes_of = {}
        bias_of = {}
        terms_of = {}
        fused_of = {}
        window_of = {}
        scaled_of = {}
        first_done = set()

        def transpose(j):
            x_chunk, place = x_of[j]
            x_words = x_chunk[:].bitcast(F32)
            xt = psum_x.tile([P, 2 * HALVES, P], F32)
            for half in range(HALVES):
                for u in range(2):
                    nc.tensor.transpose(xt[:, 2 * half + u, :], x_words[:, half, place, u:WORDS:2], identity[:])
            xt_of[j] = xt

        def regroup(j, clusters=(0, 1)):
            if j // PAIR not in grouped_of:
                grouped = quant.tile([P, PAIR, CLUSTERS * P * 4], BF16, align_bytes=64)
                grouped_of[j // PAIR] = grouped
            grouped = grouped_of[j // PAIR]
            span = slice(clusters[0], clusters[-1] + 1)
            nc.scalar.copy(
                out=grouped[:, j % PAIR, :].bitcast(F32).rearrange("p (c b s) -> p c b s", c=CLUSTERS, s=2 * HALVES)[:, span],
                in_=xt_of[j][:].rearrange("p s (b c) -> p c b s", c=CLUSTERS)[:, span],
            )

        def windows(groups):
            window = psum_acc.tile([P, BANK], F32, tag="proj")
            for place, g in enumerate(groups):
                first = CLUSTERS * GROUP * g
                nc.tensor.transpose(window[:, place * P : (place + 1) * P], probs_wide[:, first : first + P], identity[:])
            window_of[groups[0]] = window

        def windows_out(groups, engine):
            width = len(groups) * P
            engine(out=probs_t[:, groups[0] : groups[-1] + 1, :].rearrange("p g m -> p (g m)"), in_=window_of[groups[0]][:, 0:width])

        def bias_product(j):
            banks = []
            for first in range(0, E_PLAIN, BANK):
                width = min(BANK, E_PLAIN - first)
                bias_psum = psum_bias.tile([P, BANK], F32)
                nc.tensor.matmul(
                    out=bias_psum[:, 0:width], lhsT=probs_t[:, j // GROUP, :], rhs=bo_rows[:, j % GROUP, first : first + width], start=True, stop=True
                )
                banks.append((first, width, bias_psum))
            bias_psum_of[j] = banks

        def bias_tile(r):
            if r not in bias_of:
                bias = bias_pool.tile([P, PAIR, E], F32)
                bias_of[r] = bias
            return bias_of[r]

        def bias_out(j):
            for first, width, bias_psum in bias_psum_of[j]:
                nc.scalar.copy(out=bias_tile(j // PAIR)[:, j % PAIR, first : first + width], in_=bias_psum[:, 0:width])

        def rest_terms(r, tiles, on_gpsimd=(False, True), source=None):
            if r not in terms_of:
                bias0 = bias_pool.tile([P, PAIR, E_REST], F32)
                bias1 = bias_pool.tile([P, PAIR, E_REST], F32)
                terms_of[r] = (bias0, bias1)
            for t in tiles:
                j = PAIR * r + t
                for c in range(CLUSTERS):
                    rows = bo_rest[:, c, :] if source is None else source[:, c * E_REST : (c + 1) * E_REST]
                    if on_gpsimd[c]:
                        nc.gpsimd.tensor_scalar(out=terms_of[r][c][:, t, :], in0=rows, scalar1=weight(c, j), scalar2=0.0, op0=MULT, op1=ADD)
                    else:
                        nc.scalar.activation(out=terms_of[r][c][:, t, :], in_=rows, func=COPY, scale=weight(c, j))

        def rest_sum(r, tiles):
            bias0, bias1 = terms_of[r]
            span = slice(tiles[0], tiles[-1] + 1)
            nc.gpsimd.tensor_tensor(out=bias_tile(r)[:, span, E_PLAIN:E], in0=bias0[:, span, :], in1=bias1[:, span, :], op=ADD)

        def bias_rest(r, tiles, on_gpsimd=(True, True), source=None):
            rest_terms(r, tiles, on_gpsimd, source)
            rest_sum(r, tiles)

        def quantise_cluster(j, c):
            r = j // PAIR
            if r not in codes_of:
                codes = quant.tile([P, PAIR * CLUSTERS, P], U32, align_bytes=64)
                scales = quant.tile([P, PAIR * CLUSTERS, P], U8, align_bytes=64)
                codes_of[r] = (codes, scales)
            codes, scales = codes_of[r]
            slot = (j % PAIR) * CLUSTERS + c
            nc.vector.quantize_mx(
                out=codes[:, slot, :].bitcast(FP8X4),
                scales=scales[:, slot, :],
                in_=grouped_of[r][:, j % PAIR, c * P * 4 : (c + 1) * P * 4],
            )

        def quantise(r, tiles):
            if r not in codes_of:
                codes = quant.tile([P, PAIR * CLUSTERS, P], U32, align_bytes=64)
                scales = quant.tile([P, PAIR * CLUSTERS, P], U8, align_bytes=64)
                codes_of[r] = (codes, scales)
            codes, scales = codes_of[r]
            slots = slice(tiles[0] * CLUSTERS, (tiles[-1] + 1) * CLUSTERS)
            nc.vector.quantize_mx(
                out=codes[:, slots, :].rearrange("p c m -> p (c m)").bitcast(FP8X4),
                scales=scales[:, slots, :].rearrange("p c m -> p (c m)"),
                in_=grouped_of[r][:, tiles[0] : tiles[-1] + 1, :].rearrange("p t k -> p (t k)"),
            )

        def project(j, clusters, banks=(0, 1)):
            codes, scales = codes_of[j // PAIR]
            for c in clusters:
                slot = (j % PAIR) * CLUSTERS + c
                for n in banks:
                    proj = psum_acc.tile([P, BANK], F32)
                    nc.tensor.matmul_mx(
                        out=proj[:],
                        lhsT=codes[:, slot, :].bitcast(FP8X4),
                        lhsT_scale=scales[:, slot, :],
                        rhs=w_words[:, c, n * BANK : (n + 1) * BANK].bitcast(FP8X4),
                        rhs_scale=w_scales[:, c, n * BANK : (n + 1) * BANK],
                        start=True,
                        stop=True,
                    )
                    proj_of[(j, c, n)] = proj

        def mix_first(j, banks=(0, 1)):
            if j not in partial_of:
                partial = result.tile([P, E], F32)
                partial_of[j] = partial
            for n in banks:
                if (j, n) in first_done:
                    continue
                first_done.add((j, n))
                cols = slice(n * BANK, (n + 1) * BANK)
                nc.vector.scalar_tensor_tensor(
                    out=partial_of[j][:, cols], in0=proj_of[(j, 0, n)][:], scalar=weight(0, j),
                    in1=bias_of[j // PAIR][:, j % PAIR, cols], op0=MULT, op1=ADD,
                )

        def scale_bank(j, n):
            scaled = result.tile([P, BANK], F32)
            nc.scalar.activation(out=scaled[:], in_=proj_of[(j, 1, n)][:], func=COPY, scale=weight(1, j))
            scaled_of[(j, n)] = scaled

        def mix_second(j):
            if j % PAIR == 0:
                fused = result.tile([P, PAIR, E], F32)
                fused_of[j // PAIR] = fused
            fused = fused_of[j // PAIR]
            fine = j >= N_TILES - FINE_TILES
            for n in range(E_BANKS):
                pieces = (BANK - LAST_PIECE, LAST_PIECE) if (j, n) == (N_TILES - 1, E_BANKS - 1) else (BANK,)
                first = n * BANK
                for width in pieces:
                    cols = slice(first, first + width)
                    if (j, n) in scaled_of:
                        nc.gpsimd.tensor_tensor(out=fused[:, j % PAIR, cols], in0=partial_of[j][:, cols], in1=scaled_of[(j, n)][:], op=ADD)
                    else:
                        nc.vector.scalar_tensor_tensor(
                            out=fused[:, j % PAIR, cols], in0=proj_of[(j, 1, n)][:, first - n * BANK : first - n * BANK + width], scalar=weight(1, j),
                            in1=partial_of[j][:, cols], op0=MULT, op1=ADD,
                        )
                    if fine:
                        nc.sync.dma_start(out=out_rows[:, j, cols], in_=fused[:, j % PAIR, cols])
                    first += width
            if j % PAIR == PAIR - 1 and not fine:
                nc.sync.dma_start(out=out_rows[:, j - PAIR + 1 : j + 1, :], in_=fused[:])

        def live(j):
            return 0 <= j < N_TILES

        both = (0, 1)
        with tc.manual_schedule():
            nc.scalar.dma_start(out=probs_bf[:], in_=probs_rows)
            load_x(0)
            load_w(0)
            nc.vector.memset(bo_rows[:, 0, :].bitcast(I32), 0)
            nc.scalar.dma_start(out=bo_rows[0:CLUSTERS, 0, :], in_=bo[:, :])
            nc.vector.memset(w_scales[:].bitcast(I32), 0)
            load_w_scales()
            load_x(1)
            load_w(1)
            for number in range(2, EARLY_LOADS):
                load_x(number)
            nc.vector.memset(warm[:], 0.0)
            nc.scalar.activation(out=warm[:, 1:2], in_=warm[:, 0:1], func=COPY)
            make_identity(nc, identity[:])
            nc.vector.memset(probs_wide[:], 0.0)
            for t in range(1, GROUP):
                nc.vector.memset(bo_rows[:, t, 0:E_PLAIN].bitcast(I32), 0)
                nc.scalar.dma_start(out=bo_rows[CLUSTERS * t : CLUSTERS * (t + 1), t, 0:E_PLAIN], in_=bo[:, 0:E_PLAIN])
            nc.vector.tensor_copy(out=row_picker[:], in_=identity[:, 0:CLUSTERS])
            nc.vector.tensor_copy(out=probs_wide[:, 0 : N_TILES * CLUSTERS], in_=probs_bf[:])

            windows((0,))
            windows_out((0,), nc.vector.tensor_copy)
            transpose(0)
            regroup(0, (0,))
            quantise_cluster(0, 0)
            regroup(0, (1,))
            quantise_cluster(0, 1)
            spread = psum_acc.tile([P, BANK], F32, tag="proj")
            for c in range(CLUSTERS):
                nc.tensor.matmul(
                    out=spread[:, c * E_REST : (c + 1) * E_REST], lhsT=row_picker[:, c : c + 1].to_broadcast([P, P]), rhs=bo_rows[:, 0, E_PLAIN:E], start=True, stop=True
                )
            bias_product(0)
            bias_rest(0, (0,), on_gpsimd=(False, False), source=spread)
            bias_out(0)
            nc.vector.tensor_copy(out=bo_rest[:].rearrange("p c e -> p (c e)"), in_=spread[:, 0 : CLUSTERS * E_REST])
            windows((1, 2, 3))
            windows((4, 5, 6, 7))
            windows_out((1, 2, 3), nc.vector.tensor_copy)
            windows_out((4, 5, 6, 7), nc.scalar.copy)
            bias_rest(0, (1,))
            bias_rest(1, both)
            project(0, (0,))
            transpose(1)
            bias_product(1)
            regroup(1)
            mix_first(0)
            quantise(0, (1,))
            project(0, (1,))
            bias_out(1)
            mix_second(0)
            project(1, (0,))
            transpose(2)
            transpose(3)
            bias_product(2)
            project(1, (1,))
            regroup(2)
            regroup(3)
            bias_out(2)
            mix_first(1)
            quantise(1, (0,))
            mix_second(1)
            quantise(1, (1,))
            bias_rest(2, both)
            rest_terms(3, both, on_gpsimd=(True, True))
            project(2, (0,))
            transpose(4)
            transpose(5)
            bias_product(3)
            project(2, (1,))
            regroup(4)
            regroup(5)
            bias_out(3)
            bias_product(4)
            bias_out(4)
            for r in range(1, N_ROUNDS):
                a = PAIR * r
                b = a + 1
                split = r < N_ROUNDS - 1
                for number in range(EARLY_LOADS, len(X_LOADS)):
                    if first_of_load[number] == a + 4 + PAIR * LOAD_LEAD:
                        load_x(number)
                if live(a + 4):
                    transpose(a + 4)
                    transpose(a + 5)
                if not split:
                    scale_bank(a, 1)
                mix_first(a)
                mix_second(a)
                if live(a + 2):
                    quantise(r + 1, both)
                if live(a + 4):
                    regroup(a + 4)
                if split:
                    project(b, (1,), (0,))
                    scale_bank(b, 0)
                if live(a + 4):
                    regroup(a + 5)
                project(b, (0,))
                if live(a + 3):
                    bias_product(a + 3)
                    bias_out(a + 3)
                project(b, (1,), (1,) if split else (0, 1))
                mix_first(b)
                if live(a + 2):
                    project(a + 2, (0,))
                if split:
                    mix_first(a + 2, (0,))
                mix_second(b)
                if live(a + 4):
                    rest_sum(r + 2, both)
                if live(a + 6):
                    rest_terms(r + 3, (0,), on_gpsimd=(False, False))
                    rest_terms(r + 3, (1,))
                if live(a + 4):
                    bias_product(a + 4)
                    bias_out(a + 4)
                if live(a + 2):
                    project(a + 2, (1,))
